import numpy as np
import ml_dtypes


def mxq(x, axis, fmt="e4m3"):
    dtype, down = {"e4m3": (ml_dtypes.float8_e4m3fn, 7), "e5m2": (ml_dtypes.float8_e5m2, 14)}[fmt]
    v = np.moveaxis(np.asarray(x, np.float32).astype(ml_dtypes.bfloat16).astype(np.float64), axis, -1)
    blocks = v.reshape(v.shape[:-1] + (-1, 32))
    amax = np.abs(blocks).max(-1, keepdims=True)
    byte = np.maximum(np.where(amax > 0, np.frexp(amax)[1] - 1 + 127, 0) - down, 1)
    scale = np.exp2(byte - 127.0)
    codes = (blocks / scale).astype(np.float32).astype(dtype).astype(np.float64)
    return np.moveaxis((codes * scale).reshape(v.shape), -1, axis)


WIDE = False


def mx_kscale(k):
    if not WIDE:
        return np.ones(k)
    levels = np.array([10, -10, 5, -5, 0])
    a = np.random.permutation(np.resize(levels, k // 512 * 4)).reshape(k // 512, 4)
    idx = np.arange(k)
    return np.exp2(a[idx // 512, idx % 128 // 32])


BF16 = ml_dtypes.bfloat16


def bf(x):
    return np.asarray(x, np.float32).astype(BF16)


def f64(x):
    return np.asarray(x).astype(np.float64)


E2M1 = np.array([0.0, 0.5, 1.0, 1.5, 2.0, 3.0, 4.0, 6.0, -0.0, -0.5, -1.0, -1.5, -2.0, -3.0, -4.0, -6.0])


def pack_weight(w, fmt):
    k, n = w.shape
    w = f64(bf(w)).reshape(k // 32, 32, n)
    amax = np.abs(w).max(1)
    if fmt == "e4m3":
        byte = np.frexp(amax)[1] - 1 + 127 - 7
    else:
        mant, ex = np.frexp(amax / 6.0)
        byte = np.where(mant > 0.5, ex, ex - 1) + 127
    byte = np.clip(np.where(amax > 0, byte, 1), 1, 254)
    scaled = (w * np.exp2(127.0 - byte)[:, None, :]).reshape(k, n).astype(np.float32)
    by_word = np.ascontiguousarray(scaled.reshape(k // 512, 128, 4, n).transpose(0, 1, 3, 2))
    if fmt == "e4m3":
        words = by_word.astype(ml_dtypes.float8_e4m3fn).view(np.uint8)
    else:
        c = by_word.astype(ml_dtypes.float4_e2m1fn).view(np.uint8) & 0xF
        words = c[..., 0::2] | (c[..., 1::2] << 4)
    return np.ascontiguousarray(words), np.ascontiguousarray(byte.astype(np.uint8).reshape(k // 512, 16, n))


def unpack_weight(words, scales, fmt):
    g, p, n, _ = words.shape
    if fmt == "e4m3":
        vals = np.ascontiguousarray(words).view(ml_dtypes.float8_e4m3fn).astype(np.float64)
    else:
        nib = np.empty((g, p, n, 4), np.uint8)
        nib[..., 0::2] = words & 0xF
        nib[..., 1::2] = words >> 4
        vals = E2M1[nib]
    vals = vals * np.repeat(np.exp2(scales.astype(np.float64) - 127.0), 8, axis=1)[..., None]
    return vals.transpose(0, 1, 3, 2).reshape(g * 512, n)


B, S, E, H, KV, HD, HID = 2, 256, 1024, 8, 4, 128, 3072
F = (H + 2 * KV) * HD
EPS = 1e-6
ROPE_BASE = 1000000.0
FMT = "e4m3"


def rmsnorm(v, w):
    var = np.mean(v * v, axis=-1, keepdims=True)
    return v * (1.0 / np.sqrt(var + EPS)) * w


def apply_rope(v, cos, sin):
    v1 = v[..., 0::2]
    v2 = v[..., 1::2]
    r1 = v1 * cos - v2 * sin
    r2 = v1 * sin + v2 * cos
    return np.stack([r1, r2], axis=-1).reshape(v.shape)


def setup_inputs():
    s = mx_kscale(E)
    x = bf(np.random.standard_normal((B, S, E)) * 2.0)
    ln_w = bf((1.0 + 0.1 * np.random.standard_normal(E)) * s)
    qkv_w_words, qkv_w_scales = pack_weight(np.random.standard_normal((E, F)) * 2.0 / np.sqrt(E) / s[:, None], FMT)
    q_norm_w = bf(1.0 + 0.1 * np.random.standard_normal(HD))
    k_norm_w = bf(1.0 + 0.1 * np.random.standard_normal(HD))
    return {"x": x,
            "ln_w": ln_w,
            "qkv_w_words": qkv_w_words,
            "qkv_w_scales": qkv_w_scales,
            "q_norm_w": q_norm_w,
            "k_norm_w": k_norm_w}


def reference(x, ln_w, qkv_w_words, qkv_w_scales, q_norm_w, k_norm_w):
    h = rmsnorm(f64(x), f64(ln_w))
    qkv = mxq(h, 2, "e4m3") @ unpack_weight(qkv_w_words, qkv_w_scales, FMT)
    q = qkv[..., : H * HD].reshape(B, S, H, HD)
    k = qkv[..., H * HD : (H + KV) * HD].reshape(B, S, KV, HD)
    v = qkv[..., (H + KV) * HD :].reshape(B, S, KV, HD)
    q = rmsnorm(q, f64(q_norm_w))
    k = rmsnorm(k, f64(k_norm_w))
    pos = np.arange(S, dtype=np.float64)
    inv_freq = 1.0 / (ROPE_BASE ** (np.arange(0, HD, 2, dtype=np.float64) / HD))
    ang = pos[:, None] * inv_freq
    cos = np.cos(ang)[None, :, None, :]
    sin = np.sin(ang)[None, :, None, :]
    return apply_rope(q, cos, sin), apply_rope(k, cos, sin), v

@@ -1,0 +1,302 @@
+import math
+from contextlib import ExitStack
+
+import concourse.mybir as mybir
+from concourse.masks import make_identity
+
+F32 = mybir.dt.float32
+BF16 = mybir.dt.bfloat16
+I32 = mybir.dt.int32
+U32 = mybir.dt.uint32
+U8 = mybir.dt.uint8
+FP8X4 = mybir.dt.float8_e4m3fn_x4
+ALU = mybir.AluOpType
+ACT = mybir.ActivationFunctionType
+
+P = 128
+TOKENS = 512
+E = 1024
+HD = 128
+PAIRS = HD // 2
+K_PASS = 512
+PASSES = E // K_PASS
+BANK = 512
+HEADS_PER_BANK = BANK // HD
+BANKS_PER_TILE = 4
+VALUE_BANK = 3
+TILES = TOKENS // P
+JOBS = TILES * BANKS_PER_TILE
+EPS = 1e-6
+ROPE_BASE = 1000000.0
+ROUND_MAGIC = 12582912.0
+TWO_PI_HIGH = 6.28125
+TWO_PI_LOW = 2.0 * math.pi - TWO_PI_HIGH
+
+FLOPS = 2 * TOKENS * E * 2048
+
+MATMUL_AHEAD = 2
+SCALE_BEHIND = 2
+FRONT_AHEAD = 6
+TABLES_STEP = -1
+
+
+def tile_qwen3block_pa_kernel(
+    tc, x, ln_w, qkv_w_words, qkv_w_scales, q_norm_w, k_norm_w, out_0, out_1, out_2
+):
+    nc = tc.nc
+    x_rows = x.flatten_outer_dims()
+    q_rows = out_0.rearrange("b s h d -> (b s) (h d)")
+    k_rows = out_1.rearrange("b s h d -> (b s) (h d)")
+    v_rows = out_2.rearrange("b s h d -> (b s) (h d)")
+
+    with ExitStack() as stack:
+        stack.enter_context(tc.manual_schedule())
+        keep = stack.enter_context(tc.tile_pool(name="keep", bufs=1))
+        front = stack.enter_context(tc.tile_pool(name="front", bufs=2))
+        small = stack.enter_context(tc.tile_pool(name="small", bufs=6))
+        work = stack.enter_context(tc.tile_pool(name="work", bufs=4))
+        psum_t = stack.enter_context(tc.psum_pool(name="psum_t", bufs=2))
+        psum_o = stack.enter_context(tc.psum_pool(name="psum_o", bufs=6))
+
+        x_sb = keep.tile([P, TILES, E], BF16)
+        w_words = keep.tile([P, PASSES, 2048], U32, align_bytes=64)
+        w_scales = keep.tile([P, PASSES, 2048], U8, align_bytes=64)
+        ln_w_all = keep.tile([P, E], BF16)
+        head_w_all = keep.tile([P, 2, HD], BF16)
+
+        nc.vector.memset(w_scales[:].bitcast(I32), 0)
+
+        nc.scalar.dma_start(out=ln_w_all[:], in_=ln_w.partition_broadcast(P))
+        nc.scalar.dma_start(out=head_w_all[:, 0, :], in_=q_norm_w.partition_broadcast(P))
+        nc.scalar.dma_start(out=head_w_all[:, 1, :], in_=k_norm_w.partition_broadcast(P))
+
+        def load_x(i):
+            nc.sync.dma_start(out=x_sb[:, i, :], in_=x_rows[P * i : P * (i + 1), :])
+
+        def load_w(n):
+            for g in range(PASSES):
+                nc.sync.dma_start(
+                    out=w_words[:, g, BANK * n : BANK * (n + 1)].bitcast(I32),
+                    in_=qkv_w_words[g].rearrange("p n t -> p (n t)")[:, 4 * BANK * n : 4 * BANK * (n + 1)].bitcast(I32),
+                )
+
+        load_x(0)
+        load_x(1)
+        for g in range(PASSES):
+            for quadrant in range(4):
+                nc.sync.dma_start(
+                    out=w_scales[32 * quadrant : 32 * quadrant + 4, g, :].bitcast(I32),
+                    in_=qkv_w_scales[g, 4 * quadrant : 4 * quadrant + 4, :].bitcast(I32),
+                )
+        load_w(0)
+        load_x(2)
+        load_x(3)
+        load_w(1)
+        load_w(2)
+        load_w(3)
+
+        position_i = keep.tile([P, 2], I32)
+        nc.gpsimd.iota(position_i[:], pattern=[[P, 2]], base=0, channel_multiplier=1)
+        identity = keep.tile([P, P], F32)
+        make_identity(nc, identity[:])
+        eps = keep.tile([P, 1], F32)
+        nc.vector.memset(eps[:], EPS)
+
+        freq = keep.tile([P, PAIRS], F32)
+        nc.vector.memset(freq[:, 0:1], 1.0)
+        for level in range(6):
+            width = 2**level
+            nc.vector.tensor_scalar(
+                out=freq[:, width : 2 * width], in0=freq[:, 0:width],
+                scalar1=ROPE_BASE ** (-2.0 * width / HD), scalar2=None, op0=ALU.mult,
+            )
+        position = keep.tile([P, 2], F32)
+        nc.vector.tensor_copy(out=position[:], in_=position_i[:])
+        angle = keep.tile([P, 2, PAIRS], F32)
+        for b in range(2):
+            nc.vector.tensor_scalar(
+                out=angle[:, b, :], in0=freq[:], scalar1=position[:, b : b + 1], scalar2=None, op0=ALU.mult
+            )
+        turns = keep.tile([P, 2, PAIRS], F32)
+        nc.vector.tensor_scalar(
+            out=turns[:], in0=angle[:], scalar1=1.0 / (2.0 * math.pi), scalar2=ROUND_MAGIC, op0=ALU.mult, op1=ALU.add
+        )
+        nc.vector.tensor_scalar(out=turns[:], in0=turns[:], scalar1=ROUND_MAGIC, scalar2=None, op0=ALU.subtract)
+        reduced_high = keep.tile([P, 2, PAIRS], F32)
+        nc.vector.scalar_tensor_tensor(
+            out=reduced_high[:], in0=turns[:], scalar=-TWO_PI_HIGH, in1=angle[:], op0=ALU.mult, op1=ALU.add
+        )
+        sin_of = keep.tile([P, 2, 2, PAIRS], F32)
+        nc.vector.scalar_tensor_tensor(
+            out=sin_of[:, :, 1, :], in0=turns[:], scalar=-TWO_PI_LOW, in1=reduced_high[:], op0=ALU.mult, op1=ALU.add
+        )
+        magnitude = keep.tile([P, 2, PAIRS], F32)
+        nc.vector.scalar_tensor_tensor(
+            out=magnitude[:], in0=sin_of[:, :, 1, :], scalar=-1.0, in1=sin_of[:, :, 1, :], op0=ALU.mult, op1=ALU.max
+        )
+        nc.vector.tensor_scalar(
+            out=sin_of[:, :, 0, :], in0=magnitude[:], scalar1=-1.0, scalar2=math.pi / 2.0, op0=ALU.mult, op1=ALU.add
+        )
+        warm = keep.tile([P, 1], F32)
+        nc.scalar.activation(out=warm[:], in_=eps[:], func=ACT.Sqrt)
+
+        table = keep.tile([P, 2, 2, 2, 2, PAIRS], F32)
+
+        def rotation_tables():
+            trig = keep.tile([P, 2, 3, PAIRS], F32)
+            nc.scalar.activation(out=trig[:, :, 1:3, :], in_=sin_of[:], func=ACT.Sin)
+            nc.scalar.activation(out=trig[:, :, 0, :], in_=sin_of[:, :, 1, :], func=ACT.Sin, scale=-1.0)
+            for kind in range(2):
+                for member in range(2):
+                    gain = head_w_all[:, kind, :].rearrange("p (j e) -> p j e", e=2)[:, :, member]
+                    nc.gpsimd.tensor_tensor(
+                        out=table[:, kind, :, member, :, :],
+                        in0=trig[:, :, 1 - member : 3 - member, :],
+                        in1=gain.unsqueeze(1).unsqueeze(1).to_broadcast([P, 2, 2, PAIRS]),
+                        op=ALU.mult,
+                    )
+
+        h_codes = keep.tile([P, TILES, PASSES * P], U32, align_bytes=64)
+        h_scales = keep.tile([P, TILES, PASSES * P], U8, align_bytes=64)
+        x_rms_tiles = {}
+        h_tiles = {}
+        h_words = {}
+
+        def front_sum(i):
+            x_squares = front.tile([P, E], BF16)
+            x_total = small.tile([P, 1], F32)
+            nc.scalar.activation(out=x_squares[:], in_=x_sb[:, i, :], func=ACT.Square, accum_out=x_total[:])
+            x_rms = small.tile([P, 1], F32)
+            nc.scalar.activation(out=x_rms[:], in_=x_total[:], func=ACT.Sqrt, scale=1.0 / E, bias=eps[:])
+            x_rms_tiles[i] = x_rms
+
+        def front_scale_and_transpose(i):
+            x_inv_rms = small.tile([P, 1], F32)
+            nc.vector.reciprocal(out=x_inv_rms[:], in_=x_rms_tiles[i][:])
+            h = front.tile([P, E], BF16)
+            nc.vector.scalar_tensor_tensor(
+                out=h[:], in0=x_sb[:, i, :], scalar=x_inv_rms[:], in1=ln_w_all[:], op0=ALU.mult, op1=ALU.mult
+            )
+            h_t = psum_t.tile([P, PASSES, 2, P], F32)
+            for g in range(PASSES):
+                for u in range(2):
+                    nc.tensor.transpose(
+                        h_t[:, g, u, :], h[:].bitcast(F32)[:, 256 * g + u : 256 * (g + 1) : 2], identity[:]
+                    )
+            h_tiles[i] = h_t
+
+        def front_group(i):
+            grouped = front.tile([P, PASSES, P, 2], F32, align_bytes=64)
+            nc.vector.tensor_copy(out=grouped[:], in_=h_tiles[i][:].rearrange("p g u r -> p g r u"))
+            h_words[i] = grouped
+
+        def front_quantise(i):
+            nc.vector.quantize_mx(
+                out=h_codes[:, i, :].bitcast(FP8X4),
+                scales=h_scales[:, i, :],
+                in_=h_words[i][:].rearrange("p g r u -> p (g r u)").bitcast(BF16),
+            )
+
+        banks = {}
+        rotated = {}
+        inv_rms_heads = {}
+
+        def multiply(job):
+            i, n = divmod(job, BANKS_PER_TILE)
+            acc = psum_o.tile([P, BANK], F32)
+            for g in range(PASSES):
+                nc.tensor.matmul_mx(
+                    out=acc[:],
+                    lhsT=h_codes[:, i, P * g : P * (g + 1)].bitcast(FP8X4),
+                    lhsT_scale=h_scales[:, i, P * g : P * (g + 1)],
+                    rhs=w_words[:, g, BANK * n : BANK * (n + 1)].bitcast(FP8X4),
+                    rhs_scale=w_scales[:, g, BANK * n : BANK * (n + 1)],
+                    start=(g == 0),
+                    stop=(g == PASSES - 1),
+                )
+            banks[job] = acc
+
+        def store(job, result):
+            i, n = divmod(job, BANKS_PER_TILE)
+            rows = slice(P * i, P * (i + 1))
+            if n < 2:
+                nc.sync.dma_start(out=q_rows[rows, BANK * n : BANK * (n + 1)], in_=result)
+            elif n == 2:
+                nc.sync.dma_start(out=k_rows[rows, :], in_=result)
+            else:
+                nc.sync.dma_start(out=v_rows[rows, :], in_=result)
+
+        def copy_values(job):
+            values = work.tile([P, BANK], F32)
+            nc.scalar.copy(out=values[:], in_=banks[job][:])
+            store(job, values[:])
+
+        def rotate(job):
+            i, n = divmod(job, BANKS_PER_TILE)
+            acc = banks[job]
+            kind = n // 2
+            half = i % 2
+            head_squares = work.tile([P, HEADS_PER_BANK, HD], BF16)
+            head_totals = small.tile([P, HEADS_PER_BANK], F32)
+            for head in range(HEADS_PER_BANK):
+                nc.scalar.activation(
+                    out=head_squares[:, head, :], in_=acc[:, HD * head : HD * (head + 1)], func=ACT.Square,
+                    accum_out=head_totals[:, head : head + 1],
+                )
+            head_rms = small.tile([P, HEADS_PER_BANK], F32)
+            nc.scalar.activation(out=head_rms[:], in_=head_totals[:], func=ACT.Sqrt, scale=1.0 / HD, bias=eps[:])
+            head_inv_rms = small.tile([P, HEADS_PER_BANK], F32)
+            nc.vector.reciprocal(out=head_inv_rms[:], in_=head_rms[:])
+            inv_rms_heads[job] = head_inv_rms
+            pairs = acc[:].rearrange("p (h j e) -> p h j e", h=HEADS_PER_BANK, e=2)
+            shape = [P, HEADS_PER_BANK, 2, PAIRS]
+            from_a = work.tile(shape, F32)
+            nc.vector.tensor_tensor(
+                out=from_a[:],
+                in0=pairs[:, :, :, 0].unsqueeze(2).to_broadcast(shape),
+                in1=table[:, kind, half, 0, :, :].unsqueeze(1).to_broadcast(shape),
+                op=ALU.mult,
+            )
+            from_b = work.tile(shape, F32)
+            nc.vector.tensor_tensor(
+                out=from_b[:],
+                in0=pairs[:, :, :, 1].unsqueeze(2).to_broadcast(shape),
+                in1=table[:, kind, half, 1, :, :].unsqueeze(1).to_broadcast(shape),
+                op=ALU.mult,
+            )
+            planes = work.tile(shape, F32)
+            nc.gpsimd.tensor_tensor(out=planes[:], in0=from_a[:], in1=from_b[:], op=ALU.add)
+            rotated[job] = planes
+
+        def scale_and_store(job):
+            result = work.tile([P, HEADS_PER_BANK, PAIRS, 2], F32)
+            for head in range(HEADS_PER_BANK):
+                nc.scalar.activation(
+                    out=result[:, head, :, :], in_=rotated[job][:, head, :, :].rearrange("p c j -> p j c"),
+                    func=ACT.Copy, scale=inv_rms_heads[job][:, head : head + 1],
+                )
+            store(job, result[:].rearrange("p h j c -> p (h j c)"))
+
+        for step in range(-FRONT_AHEAD, JOBS + SCALE_BEHIND):
+            if 0 <= step + MATMUL_AHEAD < JOBS:
+                multiply(step + MATMUL_AHEAD)
+            for i in range(TILES):
+                first = BANKS_PER_TILE * i - FRONT_AHEAD
+                if step == first:
+                    front_sum(i)
+                if step == first + 1:
+                    front_scale_and_transpose(i)
+                if step == first + 2:
+                    front_group(i)
+                if step == first + 3:
+                    front_quantise(i)
+            if step == TABLES_STEP:
+                rotation_tables()
+            if 0 <= step < JOBS:
+                if step % BANKS_PER_TILE == VALUE_BANK:
+                    copy_values(step)
+                else:
+                    rotate(step)
+            late = step - SCALE_BEHIND
+            if 0 <= late < JOBS and late % BANKS_PER_TILE != VALUE_BANK:
+                scale_and_store(late)

@@ -29,15 +29,13 @@ JOBS = TILES * BANKS_PER_TILE
 EPS = 1e-6
 ROPE_BASE = 1000000.0
 ROUND_MAGIC = 12582912.0
-TWO_PI_HIGH = 6.28125
-TWO_PI_LOW = 2.0 * math.pi - TWO_PI_HIGH
 
 FLOPS = 2 * TOKENS * E * 2048
 
-MATMUL_AHEAD = 2
-SCALE_BEHIND = 2
-FRONT_AHEAD = 6
-TABLES_STEP = -1
+MATMUL_AHEAD = 3
+SCALE_BEHIND = 4
+FRONT_AHEAD = 7
+TABLES_STEP = -2
 
 
 def tile_qwen3block_pa_kernel(
@@ -53,20 +51,21 @@ def tile_qwen3block_pa_kernel(
         stack.enter_context(tc.manual_schedule())
         keep = stack.enter_context(tc.tile_pool(name="keep", bufs=1))
         front = stack.enter_context(tc.tile_pool(name="front", bufs=2))
-        small = stack.enter_context(tc.tile_pool(name="small", bufs=6))
-        work = stack.enter_context(tc.tile_pool(name="work", bufs=4))
+        small = stack.enter_context(tc.tile_pool(name="small", bufs=8))
+        work = stack.enter_context(tc.tile_pool(name="work", bufs=6))
         psum_t = stack.enter_context(tc.psum_pool(name="psum_t", bufs=2))
         psum_o = stack.enter_context(tc.psum_pool(name="psum_o", bufs=6))
 
         x_sb = keep.tile([P, TILES, E], BF16)
         w_words = keep.tile([P, PASSES, 2048], U32, align_bytes=64)
-        w_scales = keep.tile([P, PASSES, 2048], U8, align_bytes=64)
+        w_scales = keep.tile([P, 2048], U8, align_bytes=64)
         ln_w_all = keep.tile([P, E], BF16)
         head_w_all = keep.tile([P, 2, HD], BF16)
 
-        nc.vector.memset(w_scales[:].bitcast(I32), 0)
+        position_i = keep.tile([P, 2], I32)
+        nc.gpsimd.iota(position_i[:], pattern=[[P, 2]], base=0, channel_multiplier=1)
+        nc.gpsimd.memset(w_scales[:].bitcast(F32), 0.0)
 
-        nc.scalar.dma_start(out=ln_w_all[:], in_=ln_w.partition_broadcast(P))
         nc.scalar.dma_start(out=head_w_all[:, 0, :], in_=q_norm_w.partition_broadcast(P))
         nc.scalar.dma_start(out=head_w_all[:, 1, :], in_=k_norm_w.partition_broadcast(P))
 
@@ -74,20 +73,19 @@ def tile_qwen3block_pa_kernel(
             nc.sync.dma_start(out=x_sb[:, i, :], in_=x_rows[P * i : P * (i + 1), :])
 
         def load_w(n):
-            for g in range(PASSES):
-                nc.sync.dma_start(
-                    out=w_words[:, g, BANK * n : BANK * (n + 1)].bitcast(I32),
-                    in_=qkv_w_words[g].rearrange("p n t -> p (n t)")[:, 4 * BANK * n : 4 * BANK * (n + 1)].bitcast(I32),
-                )
+            nc.sync.dma_start(
+                out=w_words[:, :, BANK * n : BANK * (n + 1)].bitcast(I32),
+                in_=qkv_w_words.rearrange("g p n t -> p g (n t)")[:, :, 4 * BANK * n : 4 * BANK * (n + 1)].bitcast(I32),
+            )
 
         load_x(0)
         load_x(1)
-        for g in range(PASSES):
-            for quadrant in range(4):
-                nc.sync.dma_start(
-                    out=w_scales[32 * quadrant : 32 * quadrant + 4, g, :].bitcast(I32),
-                    in_=qkv_w_scales[g, 4 * quadrant : 4 * quadrant + 4, :].bitcast(I32),
-                )
+        nc.sync.dma_start(out=ln_w_all[:], in_=ln_w.partition_broadcast(P))
+        for quadrant in range(4):
+            nc.sync.dma_start(
+                out=w_scales[32 * quadrant : 32 * quadrant + 4 * PASSES, :].bitcast(I32),
+                in_=qkv_w_scales[:, 4 * quadrant : 4 * quadrant + 4, :].bitcast(I32),
+            )
         load_w(0)
         load_x(2)
         load_x(3)
@@ -95,57 +93,65 @@ def tile_qwen3block_pa_kernel(
         load_w(2)
         load_w(3)
 
-        position_i = keep.tile([P, 2], I32)
-        nc.gpsimd.iota(position_i[:], pattern=[[P, 2]], base=0, channel_multiplier=1)
         identity = keep.tile([P, P], F32)
         make_identity(nc, identity[:])
-        eps = keep.tile([P, 1], F32)
-        nc.vector.memset(eps[:], EPS)
 
-        freq = keep.tile([P, PAIRS], F32)
-        nc.vector.memset(freq[:, 0:1], 1.0)
-        for level in range(6):
+        coarse = keep.tile([P, 8], F32)
+        fine = keep.tile([P, 8], F32)
+        nc.vector.memset(coarse[:, 0:1], 1.0)
+        nc.vector.memset(fine[:, 0:1], 1.0)
+        for level in range(3):
             width = 2**level
             nc.vector.tensor_scalar(
-                out=freq[:, width : 2 * width], in0=freq[:, 0:width],
+                out=coarse[:, width : 2 * width], in0=coarse[:, 0:width],
+                scalar1=ROPE_BASE ** (-16.0 * width / HD), scalar2=None, op0=ALU.mult,
+            )
+            nc.vector.tensor_scalar(
+                out=fine[:, width : 2 * width], in0=fine[:, 0:width],
                 scalar1=ROPE_BASE ** (-2.0 * width / HD), scalar2=None, op0=ALU.mult,
             )
+        eps = keep.tile([P, 1], F32)
+        nc.vector.memset(eps[:], EPS)
         position = keep.tile([P, 2], F32)
-        nc.vector.tensor_copy(out=position[:], in_=position_i[:])
-        angle = keep.tile([P, 2, PAIRS], F32)
-        for b in range(2):
-            nc.vector.tensor_scalar(
-                out=angle[:, b, :], in0=freq[:], scalar1=position[:, b : b + 1], scalar2=None, op0=ALU.mult
-            )
-        turns = keep.tile([P, 2, PAIRS], F32)
         nc.vector.tensor_scalar(
-            out=turns[:], in0=angle[:], scalar1=1.0 / (2.0 * math.pi), scalar2=ROUND_MAGIC, op0=ALU.mult, op1=ALU.add
+            out=position[:], in0=position_i[:], scalar1=1.0 / (2.0 * math.pi), scalar2=None, op0=ALU.mult
         )
-        nc.vector.tensor_scalar(out=turns[:], in0=turns[:], scalar1=ROUND_MAGIC, scalar2=None, op0=ALU.subtract)
-        reduced_high = keep.tile([P, 2, PAIRS], F32)
+        turns = keep.tile([P, 2, 8, 8], F32)
+        for half in range(2):
+            nc.vector.scalar_tensor_tensor(
+                out=turns[:, half, :, :],
+                in0=coarse[:].unsqueeze(2).to_broadcast([P, 8, 8]),
+                scalar=position[:, half : half + 1],
+                in1=fine[:].unsqueeze(1).to_broadcast([P, 8, 8]),
+                op0=ALU.mult,
+                op1=ALU.mult,
+            )
+        shifted = keep.tile([P, 2, 8, 8], F32)
+        nc.vector.tensor_scalar(out=shifted[:], in0=turns[:], scalar1=ROUND_MAGIC, scalar2=None, op0=ALU.add)
+        minus_part = keep.tile([P, 2, PAIRS], F32)
         nc.vector.scalar_tensor_tensor(
-            out=reduced_high[:], in0=turns[:], scalar=-TWO_PI_HIGH, in1=angle[:], op0=ALU.mult, op1=ALU.add
-        )
-        sin_of = keep.tile([P, 2, 2, PAIRS], F32)
-        nc.vector.scalar_tensor_tensor(
-            out=sin_of[:, :, 1, :], in0=turns[:], scalar=-TWO_PI_LOW, in1=reduced_high[:], op0=ALU.mult, op1=ALU.add
+            out=minus_part[:], in0=shifted[:].rearrange("p b h l -> p b (h l)"), scalar=ROUND_MAGIC,
+            in1=turns[:].rearrange("p b h l -> p b (h l)"), op0=ALU.subtract, op1=ALU.subtract,
         )
         magnitude = keep.tile([P, 2, PAIRS], F32)
         nc.vector.scalar_tensor_tensor(
-            out=magnitude[:], in0=sin_of[:, :, 1, :], scalar=-1.0, in1=sin_of[:, :, 1, :], op0=ALU.mult, op1=ALU.max
+            out=magnitude[:], in0=minus_part[:], scalar=-1.0, in1=minus_part[:], op0=ALU.mult, op1=ALU.max
         )
+        quarter_less = keep.tile([P, 2, PAIRS], F32)
         nc.vector.tensor_scalar(
-            out=sin_of[:, :, 0, :], in0=magnitude[:], scalar1=-1.0, scalar2=math.pi / 2.0, op0=ALU.mult, op1=ALU.add
+            out=quarter_less[:], in0=magnitude[:], scalar1=-1.0, scalar2=0.25, op0=ALU.mult, op1=ALU.add
         )
-        warm = keep.tile([P, 1], F32)
-        nc.scalar.activation(out=warm[:], in_=eps[:], func=ACT.Sqrt)
+        warm = keep.tile([P, 2], F32)
+        nc.scalar.activation(out=warm[:, 0:1], in_=eps[:], func=ACT.Sqrt)
 
         table = keep.tile([P, 2, 2, 2, 2, PAIRS], F32)
 
         def rotation_tables():
             trig = keep.tile([P, 2, 3, PAIRS], F32)
-            nc.scalar.activation(out=trig[:, :, 1:3, :], in_=sin_of[:], func=ACT.Sin)
-            nc.scalar.activation(out=trig[:, :, 0, :], in_=sin_of[:, :, 1, :], func=ACT.Sin, scale=-1.0)
+            nc.scalar.activation(out=trig[:, :, 0, :], in_=minus_part[:], func=ACT.Sin, scale=2.0 * math.pi)
+            nc.scalar.activation(out=trig[:, :, 2, :], in_=minus_part[:], func=ACT.Sin, scale=-2.0 * math.pi)
+            nc.scalar.activation(out=trig[:, :, 1, :], in_=quarter_less[:], func=ACT.Sin, scale=2.0 * math.pi)
+            nc.scalar.activation(out=warm[:, 1:2], in_=eps[:], func=ACT.Sqrt)
             for kind in range(2):
                 for member in range(2):
                     gain = head_w_all[:, kind, :].rearrange("p (j e) -> p j e", e=2)[:, :, member]
@@ -163,7 +169,7 @@ def tile_qwen3block_pa_kernel(
         h_words = {}
 
         def front_sum(i):
-            x_squares = front.tile([P, E], BF16)
+            x_squares = work.tile([P, E], BF16)
             x_total = small.tile([P, 1], F32)
             nc.scalar.activation(out=x_squares[:], in_=x_sb[:, i, :], func=ACT.Square, accum_out=x_total[:])
             x_rms = small.tile([P, 1], F32)
@@ -210,7 +216,7 @@ def tile_qwen3block_pa_kernel(
                     lhsT=h_codes[:, i, P * g : P * (g + 1)].bitcast(FP8X4),
                     lhsT_scale=h_scales[:, i, P * g : P * (g + 1)],
                     rhs=w_words[:, g, BANK * n : BANK * (n + 1)].bitcast(FP8X4),
-                    rhs_scale=w_scales[:, g, BANK * n : BANK * (n + 1)],
+                    rhs_scale=w_scales[4 * g : P, BANK * n : BANK * (n + 1)],
                     start=(g == 0),
                     stop=(g == PASSES - 1),
                 )

@@ -33,7 +33,7 @@ ROUND_MAGIC = 12582912.0
 FLOPS = 2 * TOKENS * E * 2048
 
 MATMUL_AHEAD = 3
-SCALE_BEHIND = 4
+ROTATE_BEHIND = 1
 FRONT_AHEAD = 7
 TABLES_STEP = -2
 
@@ -144,7 +144,7 @@ def tile_qwen3block_pa_kernel(
         warm = keep.tile([P, 2], F32)
         nc.scalar.activation(out=warm[:, 0:1], in_=eps[:], func=ACT.Sqrt)
 
-        table = keep.tile([P, 2, 2, 2, 2, PAIRS], F32)
+        table = keep.tile([P, 2, 2, PAIRS, 2, 2], F32)
 
         def rotation_tables():
             trig = keep.tile([P, 2, 3, PAIRS], F32)
@@ -156,9 +156,9 @@ def tile_qwen3block_pa_kernel(
                 for member in range(2):
                     gain = head_w_all[:, kind, :].rearrange("p (j e) -> p j e", e=2)[:, :, member]
                     nc.gpsimd.tensor_tensor(
-                        out=table[:, kind, :, member, :, :],
-                        in0=trig[:, :, 1 - member : 3 - member, :],
-                        in1=gain.unsqueeze(1).unsqueeze(1).to_broadcast([P, 2, 2, PAIRS]),
+                        out=table[:, kind, :, :, member, :],
+                        in0=trig[:, :, 1 - member : 3 - member, :].rearrange("p b c j -> p b j c"),
+                        in1=gain.unsqueeze(1).unsqueeze(3).to_broadcast([P, 2, PAIRS, 2]),
                         op=ALU.mult,
                     )
 
@@ -204,8 +204,7 @@ def tile_qwen3block_pa_kernel(
             )
 
         banks = {}
-        rotated = {}
-        inv_rms_heads = {}
+        totals = {}
 
         def multiply(job):
             i, n = divmod(job, BANKS_PER_TILE)
@@ -237,11 +236,8 @@ def tile_qwen3block_pa_kernel(
             nc.scalar.copy(out=values[:], in_=banks[job][:])
             store(job, values[:])
 
-        def rotate(job):
-            i, n = divmod(job, BANKS_PER_TILE)
+        def sum_squares(job):
             acc = banks[job]
-            kind = n // 2
-            half = i % 2
             head_squares = work.tile([P, HEADS_PER_BANK, HD], BF16)
             head_totals = small.tile([P, HEADS_PER_BANK], F32)
             for head in range(HEADS_PER_BANK):
@@ -249,41 +245,32 @@ def tile_qwen3block_pa_kernel(
                     out=head_squares[:, head, :], in_=acc[:, HD * head : HD * (head + 1)], func=ACT.Square,
                     accum_out=head_totals[:, head : head + 1],
                 )
+            totals[job] = head_totals
+
+        def rotate(job):
+            i, n = divmod(job, BANKS_PER_TILE)
+            kind = n // 2
+            half = i % 2
             head_rms = small.tile([P, HEADS_PER_BANK], F32)
-            nc.scalar.activation(out=head_rms[:], in_=head_totals[:], func=ACT.Sqrt, scale=1.0 / HD, bias=eps[:])
+            nc.scalar.activation(out=head_rms[:], in_=totals[job][:], func=ACT.Sqrt, scale=1.0 / HD, bias=eps[:])
             head_inv_rms = small.tile([P, HEADS_PER_BANK], F32)
             nc.vector.reciprocal(out=head_inv_rms[:], in_=head_rms[:])
-            inv_rms_heads[job] = head_inv_rms
-            pairs = acc[:].rearrange("p (h j e) -> p h j e", h=HEADS_PER_BANK, e=2)
-            shape = [P, HEADS_PER_BANK, 2, PAIRS]
-            from_a = work.tile(shape, F32)
-            nc.vector.tensor_tensor(
-                out=from_a[:],
-                in0=pairs[:, :, :, 0].unsqueeze(2).to_broadcast(shape),
-                in1=table[:, kind, half, 0, :, :].unsqueeze(1).to_broadcast(shape),
-                op=ALU.mult,
-            )
-            from_b = work.tile(shape, F32)
-            nc.vector.tensor_tensor(
-                out=from_b[:],
-                in0=pairs[:, :, :, 1].unsqueeze(2).to_broadcast(shape),
-                in1=table[:, kind, half, 1, :, :].unsqueeze(1).to_broadcast(shape),
-                op=ALU.mult,
-            )
-            planes = work.tile(shape, F32)
-            nc.gpsimd.tensor_tensor(out=planes[:], in0=from_a[:], in1=from_b[:], op=ALU.add)
-            rotated[job] = planes
-
-        def scale_and_store(job):
-            result = work.tile([P, HEADS_PER_BANK, PAIRS, 2], F32)
+            products = work.tile([P, HEADS_PER_BANK, PAIRS, 2, 2], F32)
             for head in range(HEADS_PER_BANK):
-                nc.scalar.activation(
-                    out=result[:, head, :, :], in_=rotated[job][:, head, :, :].rearrange("p c j -> p j c"),
-                    func=ACT.Copy, scale=inv_rms_heads[job][:, head : head + 1],
+                nc.vector.scalar_tensor_tensor(
+                    out=products[:, head, :, :, :].rearrange("p j m c -> p (j m) c"),
+                    in0=banks[job][:, HD * head : HD * (head + 1)].unsqueeze(2).to_broadcast([P, HD, 2]),
+                    scalar=head_inv_rms[:, head : head + 1],
+                    in1=table[:, kind, half, :, :, :].rearrange("p j m c -> p (j m) c"),
+                    op0=ALU.mult,
+                    op1=ALU.mult,
                 )
-            store(job, result[:].rearrange("p h j c -> p (h j c)"))
+            result = work.tile([P, HEADS_PER_BANK * PAIRS, 2], F32)
+            by_pair = products[:].rearrange("p h j m c -> p (h j) m c")
+            nc.gpsimd.tensor_tensor(out=result[:], in0=by_pair[:, :, 0, :], in1=by_pair[:, :, 1, :], op=ALU.add)
+            store(job, result[:].rearrange("p q c -> p (q c)"))
 
-        for step in range(-FRONT_AHEAD, JOBS + SCALE_BEHIND):
+        for step in range(-FRONT_AHEAD, JOBS + ROTATE_BEHIND):
             if 0 <= step + MATMUL_AHEAD < JOBS:
                 multiply(step + MATMUL_AHEAD)
             for i in range(TILES):
@@ -302,7 +289,7 @@ def tile_qwen3block_pa_kernel(
                 if step % BANKS_PER_TILE == VALUE_BANK:
                     copy_values(step)
                 else:
-                    rotate(step)
-            late = step - SCALE_BEHIND
+                    sum_squares(step)
+            late = step - ROTATE_BEHIND
             if 0 <= late < JOBS and late % BANKS_PER_TILE != VALUE_BANK:
-                scale_and_store(late)
+                rotate(late)

@@ -267,7 +267,7 @@ def tile_qwen3block_pa_kernel(
                 )
             result = work.tile([P, HEADS_PER_BANK * PAIRS, 2], F32)
             by_pair = products[:].rearrange("p h j m c -> p (h j) m c")
-            nc.gpsimd.tensor_tensor(out=result[:], in0=by_pair[:, :, 0, :], in1=by_pair[:, :, 1, :], op=ALU.add)
+            nc.vector.tensor_tensor(out=result[:], in0=by_pair[:, :, 0, :], in1=by_pair[:, :, 1, :], op=ALU.add)
             store(job, result[:].rearrange("p q c -> p (q c)"))
 
         for step in range(-FRONT_AHEAD, JOBS + ROTATE_BEHIND):

@@ -33,9 +33,10 @@ ROUND_MAGIC = 12582912.0
 FLOPS = 2 * TOKENS * E * 2048
 
 MATMUL_AHEAD = 3
-ROTATE_BEHIND = 1
-FRONT_AHEAD = 7
-TABLES_STEP = -2
+INVERT_BEHIND = 1
+ROTATE_BEHIND = 2
+FRONT_AHEAD = 8
+TABLES_STEP = -3
 
 
 def tile_qwen3block_pa_kernel(
@@ -165,6 +166,7 @@ def tile_qwen3block_pa_kernel(
         h_codes = keep.tile([P, TILES, PASSES * P], U32, align_bytes=64)
         h_scales = keep.tile([P, TILES, PASSES * P], U8, align_bytes=64)
         x_rms_tiles = {}
+        x_inv_rms_tiles = {}
         h_tiles = {}
         h_words = {}
 
@@ -176,12 +178,15 @@ def tile_qwen3block_pa_kernel(
             nc.scalar.activation(out=x_rms[:], in_=x_total[:], func=ACT.Sqrt, scale=1.0 / E, bias=eps[:])
             x_rms_tiles[i] = x_rms
 
-        def front_scale_and_transpose(i):
+        def front_invert(i):
             x_inv_rms = small.tile([P, 1], F32)
             nc.vector.reciprocal(out=x_inv_rms[:], in_=x_rms_tiles[i][:])
+            x_inv_rms_tiles[i] = x_inv_rms
+
+        def front_scale_and_transpose(i):
             h = front.tile([P, E], BF16)
             nc.vector.scalar_tensor_tensor(
-                out=h[:], in0=x_sb[:, i, :], scalar=x_inv_rms[:], in1=ln_w_all[:], op0=ALU.mult, op1=ALU.mult
+                out=h[:], in0=x_sb[:, i, :], scalar=x_inv_rms_tiles[i][:], in1=ln_w_all[:], op0=ALU.mult, op1=ALU.mult
             )
             h_t = psum_t.tile([P, PASSES, 2, P], F32)
             for g in range(PASSES):
@@ -205,6 +210,7 @@ def tile_qwen3block_pa_kernel(
 
         banks = {}
         totals = {}
+        inv_rms = {}
 
         def multiply(job):
             i, n = divmod(job, BANKS_PER_TILE)
@@ -247,14 +253,18 @@ def tile_qwen3block_pa_kernel(
                 )
             totals[job] = head_totals
 
-        def rotate(job):
-            i, n = divmod(job, BANKS_PER_TILE)
-            kind = n // 2
-            half = i % 2
+        def invert_rms(job):
             head_rms = small.tile([P, HEADS_PER_BANK], F32)
             nc.scalar.activation(out=head_rms[:], in_=totals[job][:], func=ACT.Sqrt, scale=1.0 / HD, bias=eps[:])
             head_inv_rms = small.tile([P, HEADS_PER_BANK], F32)
             nc.vector.reciprocal(out=head_inv_rms[:], in_=head_rms[:])
+            inv_rms[job] = head_inv_rms
+
+        def rotate(job):
+            i, n = divmod(job, BANKS_PER_TILE)
+            kind = n // 2
+            half = i % 2
+            head_inv_rms = inv_rms[job]
             products = work.tile([P, HEADS_PER_BANK, PAIRS, 2, 2], F32)
             for head in range(HEADS_PER_BANK):
                 nc.vector.scalar_tensor_tensor(
@@ -267,8 +277,12 @@ def tile_qwen3block_pa_kernel(
                 )
             result = work.tile([P, HEADS_PER_BANK * PAIRS, 2], F32)
             by_pair = products[:].rearrange("p h j m c -> p (h j) m c")
-            nc.vector.tensor_tensor(out=result[:], in0=by_pair[:, :, 0, :], in1=by_pair[:, :, 1, :], op=ALU.add)
+            adder = nc.vector if kind == 1 else nc.gpsimd
+            adder.tensor_tensor(out=result[:], in0=by_pair[:, :, 0, :], in1=by_pair[:, :, 1, :], op=ALU.add)
             store(job, result[:].rearrange("p q c -> p (q c)"))
+
+        def is_rotated(job):
+            return 0 <= job < JOBS and job % BANKS_PER_TILE != VALUE_BANK
 
         for step in range(-FRONT_AHEAD, JOBS + ROTATE_BEHIND):
             if 0 <= step + MATMUL_AHEAD < JOBS:
@@ -278,18 +292,20 @@ def tile_qwen3block_pa_kernel(
                 if step == first:
                     front_sum(i)
                 if step == first + 1:
-                    front_scale_and_transpose(i)
+                    front_invert(i)
                 if step == first + 2:
-                    front_group(i)
+                    front_scale_and_transpose(i)
                 if step == first + 3:
+                    front_group(i)
+                if step == first + 4:
                     front_quantise(i)
             if step == TABLES_STEP:
                 rotation_tables()
-            if 0 <= step < JOBS:
-                if step % BANKS_PER_TILE == VALUE_BANK:
-                    copy_values(step)
-                else:
-                    sum_squares(step)
-            late = step - ROTATE_BEHIND
-            if 0 <= late < JOBS and late % BANKS_PER_TILE != VALUE_BANK:
-                rotate(late)
+            if is_rotated(step):
+                sum_squares(step)
+            elif 0 <= step < JOBS:
+                copy_values(step)
+            if is_rotated(step - INVERT_BEHIND):
+                invert_rms(step - INVERT_BEHIND)
+            if is_rotated(step - ROTATE_BEHIND):
+                rotate(step - ROTATE_BEHIND)

@@ -143,7 +143,7 @@ def tile_qwen3block_pa_kernel(
             out=quarter_less[:], in0=magnitude[:], scalar1=-1.0, scalar2=0.25, op0=ALU.mult, op1=ALU.add
         )
         warm = keep.tile([P, 2], F32)
-        nc.scalar.activation(out=warm[:, 0:1], in_=eps[:], func=ACT.Sqrt)
+        nc.scalar.activation(out=warm[:, 0:1], in_=eps[:], func=ACT.Abs_reciprocal_sqrt)
 
         table = keep.tile([P, 2, 2, PAIRS, 2, 2], F32)
 
@@ -152,7 +152,7 @@ def tile_qwen3block_pa_kernel(
             nc.scalar.activation(out=trig[:, :, 0, :], in_=minus_part[:], func=ACT.Sin, scale=2.0 * math.pi)
             nc.scalar.activation(out=trig[:, :, 2, :], in_=minus_part[:], func=ACT.Sin, scale=-2.0 * math.pi)
             nc.scalar.activation(out=trig[:, :, 1, :], in_=quarter_less[:], func=ACT.Sin, scale=2.0 * math.pi)
-            nc.scalar.activation(out=warm[:, 1:2], in_=eps[:], func=ACT.Sqrt)
+            nc.scalar.activation(out=warm[:, 1:2], in_=eps[:], func=ACT.Abs_reciprocal_sqrt)
             for kind in range(2):
                 for member in range(2):
                     gain = head_w_all[:, kind, :].rearrange("p (j e) -> p j e", e=2)[:, :, member]
@@ -165,7 +165,6 @@ def tile_qwen3block_pa_kernel(
 
         h_codes = keep.tile([P, TILES, PASSES * P], U32, align_bytes=64)
         h_scales = keep.tile([P, TILES, PASSES * P], U8, align_bytes=64)
-        x_rms_tiles = {}
         x_inv_rms_tiles = {}
         h_tiles = {}
         h_words = {}
@@ -174,13 +173,10 @@ def tile_qwen3block_pa_kernel(
             x_squares = work.tile([P, E], BF16)
             x_total = small.tile([P, 1], F32)
             nc.scalar.activation(out=x_squares[:], in_=x_sb[:, i, :], func=ACT.Square, accum_out=x_total[:])
-            x_rms = small.tile([P, 1], F32)
-            nc.scalar.activation(out=x_rms[:], in_=x_total[:], func=ACT.Sqrt, scale=1.0 / E, bias=eps[:])
-            x_rms_tiles[i] = x_rms
-
-        def front_invert(i):
             x_inv_rms = small.tile([P, 1], F32)
-            nc.vector.reciprocal(out=x_inv_rms[:], in_=x_rms_tiles[i][:])
+            nc.scalar.activation(
+                out=x_inv_rms[:], in_=x_total[:], func=ACT.Abs_reciprocal_sqrt, scale=1.0 / E, bias=eps[:]
+            )
             x_inv_rms_tiles[i] = x_inv_rms
 
         def front_scale_and_transpose(i):
@@ -254,10 +250,10 @@ def tile_qwen3block_pa_kernel(
             totals[job] = head_totals
 
         def invert_rms(job):
-            head_rms = small.tile([P, HEADS_PER_BANK], F32)
-            nc.scalar.activation(out=head_rms[:], in_=totals[job][:], func=ACT.Sqrt, scale=1.0 / HD, bias=eps[:])
             head_inv_rms = small.tile([P, HEADS_PER_BANK], F32)
-            nc.vector.reciprocal(out=head_inv_rms[:], in_=head_rms[:])
+            nc.scalar.activation(
+                out=head_inv_rms[:], in_=totals[job][:], func=ACT.Abs_reciprocal_sqrt, scale=1.0 / HD, bias=eps[:]
+            )
             inv_rms[job] = head_inv_rms
 
         def rotate(job):
@@ -291,8 +287,6 @@ def tile_qwen3block_pa_kernel(
                 first = BANKS_PER_TILE * i - FRONT_AHEAD
                 if step == first:
                     front_sum(i)
-                if step == first + 1:
-                    front_invert(i)
                 if step == first + 2:
                     front_scale_and_transpose(i)
                 if step == first + 3:

@@ -54,21 +54,24 @@ def tile_qwen3block_pa_kernel(
         front = stack.enter_context(tc.tile_pool(name="front", bufs=2))
         small = stack.enter_context(tc.tile_pool(name="small", bufs=8))
         work = stack.enter_context(tc.tile_pool(name="work", bufs=6))
-        psum_t = stack.enter_context(tc.psum_pool(name="psum_t", bufs=2))
-        psum_o = stack.enter_context(tc.psum_pool(name="psum_o", bufs=6))
+        psum_g = stack.enter_context(tc.psum_pool(name="psum_g", bufs=1))
+        psum_t = stack.enter_context(tc.psum_pool(name="psum_t", bufs=1))
+        psum_o = stack.enter_context(tc.psum_pool(name="psum_o", bufs=5))
 
         x_sb = keep.tile([P, TILES, E], BF16)
         w_words = keep.tile([P, PASSES, 2048], U32, align_bytes=64)
         w_scales = keep.tile([P, 2048], U8, align_bytes=64)
-        ln_w_all = keep.tile([P, E], BF16)
         head_w_all = keep.tile([P, 2, HD], BF16)
+
+        gain_rows = keep.tile([P, E + 2 * HD], BF16)
+        nc.gpsimd.memset(gain_rows[:].bitcast(F32), 0.0)
+        ones = keep.tile([P, P], BF16)
+        nc.vector.memset(ones[:], 1.0)
 
         position_i = keep.tile([P, 2], I32)
         nc.gpsimd.iota(position_i[:], pattern=[[P, 2]], base=0, channel_multiplier=1)
         nc.gpsimd.memset(w_scales[:].bitcast(F32), 0.0)
 
-        nc.scalar.dma_start(out=head_w_all[:, 0, :], in_=q_norm_w.partition_broadcast(P))
-        nc.scalar.dma_start(out=head_w_all[:, 1, :], in_=k_norm_w.partition_broadcast(P))
 
         def load_x(i):
             nc.sync.dma_start(out=x_sb[:, i, :], in_=x_rows[P * i : P * (i + 1), :])
@@ -80,8 +83,10 @@ def tile_qwen3block_pa_kernel(
             )
 
         load_x(0)
+        nc.sync.dma_start(out=gain_rows[0:1, 0:E], in_=ln_w.unsqueeze(0))
+        nc.sync.dma_start(out=gain_rows[0:1, E : E + HD], in_=q_norm_w.unsqueeze(0))
+        nc.sync.dma_start(out=gain_rows[0:1, E + HD : E + 2 * HD], in_=k_norm_w.unsqueeze(0))
         load_x(1)
-        nc.sync.dma_start(out=ln_w_all[:], in_=ln_w.partition_broadcast(P))
         for quadrant in range(4):
             nc.sync.dma_start(
                 out=w_scales[32 * quadrant : 32 * quadrant + 4 * PASSES, :].bitcast(I32),
@@ -163,6 +168,19 @@ def tile_qwen3block_pa_kernel(
                         op=ALU.mult,
                     )
 
+        ln_w_all = []
+        for g in range(PASSES):
+            ln_w_bank = psum_g.tile([P, K_PASS], F32, name="ln_w_bank%d" % g)
+            nc.tensor.matmul(
+                out=ln_w_bank[:], lhsT=ones[:], rhs=gain_rows[:, K_PASS * g : K_PASS * (g + 1)], start=True, stop=True
+            )
+            ln_w_all.append(ln_w_bank)
+        head_w_bank = psum_t.tile([P, BANK], F32, tag="turned")
+        nc.tensor.matmul(
+            out=head_w_bank[:, 0 : 2 * HD], lhsT=ones[:], rhs=gain_rows[:, E : E + 2 * HD], start=True, stop=True
+        )
+        nc.vector.tensor_copy(out=head_w_all[:].rearrange("p k d -> p (k d)"), in_=head_w_bank[:, 0 : 2 * HD])
+
         h_codes = keep.tile([P, TILES, PASSES * P], U32, align_bytes=64)
         h_scales = keep.tile([P, TILES, PASSES * P], U8, align_bytes=64)
         x_inv_rms_tiles = {}
@@ -181,10 +199,13 @@ def tile_qwen3block_pa_kernel(
 
         def front_scale_and_transpose(i):
             h = front.tile([P, E], BF16)
-            nc.vector.scalar_tensor_tensor(
-                out=h[:], in0=x_sb[:, i, :], scalar=x_inv_rms_tiles[i][:], in1=ln_w_all[:], op0=ALU.mult, op1=ALU.mult
-            )
-            h_t = psum_t.tile([P, PASSES, 2, P], F32)
+            for g in range(PASSES):
+                k_cols = slice(K_PASS * g, K_PASS * (g + 1))
+                nc.vector.scalar_tensor_tensor(
+                    out=h[:, k_cols], in0=x_sb[:, i, k_cols], scalar=x_inv_rms_tiles[i][:], in1=ln_w_all[g][:],
+                    op0=ALU.mult, op1=ALU.mult,
+                )
+            h_t = psum_t.tile([P, PASSES, 2, P], F32, tag="turned")
             for g in range(PASSES):
                 for u in range(2):
                     nc.tensor.transpose(

@@ -22,10 +22,11 @@ K_PASS = 512
 PASSES = E // K_PASS
 BANK = 512
 HEADS_PER_BANK = BANK // HD
-BANKS_PER_TILE = 4
+ROTATED_BANKS = 3
 VALUE_BANK = 3
 TILES = TOKENS // P
-JOBS = TILES * BANKS_PER_TILE
+JOBS = [(i, n) for i in range(TILES) for n in range(ROTATED_BANKS)] + [(i, VALUE_BANK) for i in range(TILES)]
+ROTATED_JOBS = TILES * ROTATED_BANKS
 EPS = 1e-6
 ROPE_BASE = 1000000.0
 ROUND_MAGIC = 12582912.0
@@ -33,10 +34,11 @@ ROUND_MAGIC = 12582912.0
 FLOPS = 2 * TOKENS * E * 2048
 
 MATMUL_AHEAD = 3
-INVERT_BEHIND = 1
-ROTATE_BEHIND = 2
-FRONT_AHEAD = 8
-TABLES_STEP = -3
+SUM_AHEAD = 2
+INVERT_AHEAD = 1
+QUANTISE_AHEAD = 3
+GROUP_AHEAD = 4
+TRANSPOSE_AHEAD = 6
 
 
 def tile_qwen3block_pa_kernel(
@@ -51,12 +53,11 @@ def tile_qwen3block_pa_kernel(
     with ExitStack() as stack:
         stack.enter_context(tc.manual_schedule())
         keep = stack.enter_context(tc.tile_pool(name="keep", bufs=1))
-        front = stack.enter_context(tc.tile_pool(name="front", bufs=2))
+        front = stack.enter_context(tc.tile_pool(name="front", bufs=TILES))
         small = stack.enter_context(tc.tile_pool(name="small", bufs=8))
         work = stack.enter_context(tc.tile_pool(name="work", bufs=6))
-        psum_g = stack.enter_context(tc.psum_pool(name="psum_g", bufs=1))
         psum_t = stack.enter_context(tc.psum_pool(name="psum_t", bufs=1))
-        psum_o = stack.enter_context(tc.psum_pool(name="psum_o", bufs=5))
+        psum_o = stack.enter_context(tc.psum_pool(name="psum_o", bufs=7))
 
         x_sb = keep.tile([P, TILES, E], BF16)
         w_words = keep.tile([P, PASSES, 2048], U32, align_bytes=64)
@@ -87,14 +88,14 @@ def tile_qwen3block_pa_kernel(
         nc.sync.dma_start(out=gain_rows[0:1, E : E + HD], in_=q_norm_w.unsqueeze(0))
         nc.sync.dma_start(out=gain_rows[0:1, E + HD : E + 2 * HD], in_=k_norm_w.unsqueeze(0))
         load_x(1)
+        load_x(2)
+        load_x(3)
         for quadrant in range(4):
             nc.sync.dma_start(
                 out=w_scales[32 * quadrant : 32 * quadrant + 4 * PASSES, :].bitcast(I32),
                 in_=qkv_w_scales[:, 4 * quadrant : 4 * quadrant + 4, :].bitcast(I32),
             )
         load_w(0)
-        load_x(2)
-        load_x(3)
         load_w(1)
         load_w(2)
         load_w(3)
@@ -102,6 +103,10 @@ def tile_qwen3block_pa_kernel(
         identity = keep.tile([P, P], F32)
         make_identity(nc, identity[:])
 
+        eps = keep.tile([P, 1], F32)
+        nc.vector.memset(eps[:], EPS)
+        warm = keep.tile([P, 2], F32)
+        nc.scalar.activation(out=warm[:, 0:1], in_=eps[:], func=ACT.Sin)
         coarse = keep.tile([P, 8], F32)
         fine = keep.tile([P, 8], F32)
         nc.vector.memset(coarse[:, 0:1], 1.0)
@@ -116,8 +121,6 @@ def tile_qwen3block_pa_kernel(
                 out=fine[:, width : 2 * width], in0=fine[:, 0:width],
                 scalar1=ROPE_BASE ** (-2.0 * width / HD), scalar2=None, op0=ALU.mult,
             )
-        eps = keep.tile([P, 1], F32)
-        nc.vector.memset(eps[:], EPS)
         position = keep.tile([P, 2], F32)
         nc.vector.tensor_scalar(
             out=position[:], in0=position_i[:], scalar1=1.0 / (2.0 * math.pi), scalar2=None, op0=ALU.mult
@@ -134,30 +137,30 @@ def tile_qwen3block_pa_kernel(
             )
         shifted = keep.tile([P, 2, 8, 8], F32)
         nc.vector.tensor_scalar(out=shifted[:], in0=turns[:], scalar1=ROUND_MAGIC, scalar2=None, op0=ALU.add)
-        minus_part = keep.tile([P, 2, PAIRS], F32)
+        sin_of = keep.tile([P, 2, 3, PAIRS], F32)
+        minus_part = sin_of[:, :, 0, :]
         nc.vector.scalar_tensor_tensor(
-            out=minus_part[:], in0=shifted[:].rearrange("p b h l -> p b (h l)"), scalar=ROUND_MAGIC,
+            out=minus_part, in0=shifted[:].rearrange("p b h l -> p b (h l)"), scalar=ROUND_MAGIC,
             in1=turns[:].rearrange("p b h l -> p b (h l)"), op0=ALU.subtract, op1=ALU.subtract,
         )
         magnitude = keep.tile([P, 2, PAIRS], F32)
         nc.vector.scalar_tensor_tensor(
-            out=magnitude[:], in0=minus_part[:], scalar=-1.0, in1=minus_part[:], op0=ALU.mult, op1=ALU.max
+            out=magnitude[:], in0=minus_part, scalar=-1.0, in1=minus_part, op0=ALU.mult, op1=ALU.max
         )
-        quarter_less = keep.tile([P, 2, PAIRS], F32)
         nc.vector.tensor_scalar(
-            out=quarter_less[:], in0=magnitude[:], scalar1=-1.0, scalar2=0.25, op0=ALU.mult, op1=ALU.add
+            out=sin_of[:, :, 1, :], in0=magnitude[:], scalar1=-1.0, scalar2=0.25, op0=ALU.mult, op1=ALU.add
         )
-        warm = keep.tile([P, 2], F32)
-        nc.scalar.activation(out=warm[:, 0:1], in_=eps[:], func=ACT.Abs_reciprocal_sqrt)
+        nc.vector.tensor_scalar(out=sin_of[:, :, 2, :], in0=minus_part, scalar1=-1.0, scalar2=None, op0=ALU.mult)
+        trig = keep.tile([P, 2, 3, PAIRS], F32)
+        nc.scalar.activation(
+            out=trig[:].rearrange("p b c j -> p (b c j)"), in_=sin_of[:].rearrange("p b c j -> p (b c j)"),
+            func=ACT.Sin, scale=2.0 * math.pi,
+        )
+        nc.scalar.activation(out=warm[:, 1:2], in_=eps[:], func=ACT.Abs_reciprocal_sqrt)
 
         table = keep.tile([P, 2, 2, PAIRS, 2, 2], F32)
 
         def rotation_tables():
-            trig = keep.tile([P, 2, 3, PAIRS], F32)
-            nc.scalar.activation(out=trig[:, :, 0, :], in_=minus_part[:], func=ACT.Sin, scale=2.0 * math.pi)
-            nc.scalar.activation(out=trig[:, :, 2, :], in_=minus_part[:], func=ACT.Sin, scale=-2.0 * math.pi)
-            nc.scalar.activation(out=trig[:, :, 1, :], in_=quarter_less[:], func=ACT.Sin, scale=2.0 * math.pi)
-            nc.scalar.activation(out=warm[:, 1:2], in_=eps[:], func=ACT.Abs_reciprocal_sqrt)
             for kind in range(2):
                 for member in range(2):
                     gain = head_w_all[:, kind, :].rearrange("p (j e) -> p j e", e=2)[:, :, member]
@@ -169,17 +172,20 @@ def tile_qwen3block_pa_kernel(
                     )
 
         ln_w_all = []
-        for g in range(PASSES):
-            ln_w_bank = psum_g.tile([P, K_PASS], F32, name="ln_w_bank%d" % g)
+
+        def spread_gains():
+            for g in range(PASSES):
+                ln_w_bank = psum_o.tile([P, K_PASS], F32, tag="bank")
+                nc.tensor.matmul(
+                    out=ln_w_bank[:], lhsT=ones[:], rhs=gain_rows[:, K_PASS * g : K_PASS * (g + 1)], start=True, stop=True
+                )
+                ln_w_all.append(ln_w_bank)
+            head_w_bank = psum_t.tile([P, BANK], F32, tag="turned")
             nc.tensor.matmul(
-                out=ln_w_bank[:], lhsT=ones[:], rhs=gain_rows[:, K_PASS * g : K_PASS * (g + 1)], start=True, stop=True
+                out=head_w_bank[:, 0 : 2 * HD], lhsT=ones[:], rhs=gain_rows[:, E : E + 2 * HD], start=True, stop=True
             )
-            ln_w_all.append(ln_w_bank)
-        head_w_bank = psum_t.tile([P, BANK], F32, tag="turned")
-        nc.tensor.matmul(
-            out=head_w_bank[:, 0 : 2 * HD], lhsT=ones[:], rhs=gain_rows[:, E : E + 2 * HD], start=True, stop=True
-        )
-        nc.vector.tensor_copy(out=head_w_all[:].rearrange("p k d -> p (k d)"), in_=head_w_bank[:, 0 : 2 * HD])
+            nc.vector.tensor_copy(out=head_w_all[:].rearrange("p k d -> p (k d)"), in_=head_w_bank[:, 0 : 2 * HD])
+            rotation_tables()
 
         h_codes = keep.tile([P, TILES, PASSES * P], U32, align_bytes=64)
         h_scales = keep.tile([P, TILES, PASSES * P], U8, align_bytes=64)
@@ -190,14 +196,22 @@ def tile_qwen3block_pa_kernel(
         def front_sum(i):
             x_squares = work.tile([P, E], BF16)
             x_total = small.tile([P, 1], F32)
-            nc.scalar.activation(out=x_squares[:], in_=x_sb[:, i, :], func=ACT.Square, accum_out=x_total[:])
+            if i == 0:
+                nc.vector.scalar_tensor_tensor(
+                    out=x_squares[:], in0=x_sb[:, i, :], scalar=1.0, in1=x_sb[:, i, :], op0=ALU.mult, op1=ALU.mult,
+                    accum_out=x_total[:],
+                )
+            else:
+                nc.scalar.activation(out=x_squares[:], in_=x_sb[:, i, :], func=ACT.Square, accum_out=x_total[:])
             x_inv_rms = small.tile([P, 1], F32)
             nc.scalar.activation(
                 out=x_inv_rms[:], in_=x_total[:], func=ACT.Abs_reciprocal_sqrt, scale=1.0 / E, bias=eps[:]
             )
             x_inv_rms_tiles[i] = x_inv_rms
 
-        def front_scale_and_transpose(i):
+        h_rows = {}
+
+        def front_scale(i):
             h = front.tile([P, E], BF16)
             for g in range(PASSES):
                 k_cols = slice(K_PASS * g, K_PASS * (g + 1))
@@ -205,6 +219,10 @@ def tile_qwen3block_pa_kernel(
                     out=h[:, k_cols], in0=x_sb[:, i, k_cols], scalar=x_inv_rms_tiles[i][:], in1=ln_w_all[g][:],
                     op0=ALU.mult, op1=ALU.mult,
                 )
+            h_rows[i] = h
+
+        def front_transpose(i):
+            h = h_rows[i]
             h_t = psum_t.tile([P, PASSES, 2, P], F32, tag="turned")
             for g in range(PASSES):
                 for u in range(2):
@@ -215,7 +233,7 @@ def tile_qwen3block_pa_kernel(
 
         def front_group(i):
             grouped = front.tile([P, PASSES, P, 2], F32, align_bytes=64)
-            nc.vector.tensor_copy(out=grouped[:], in_=h_tiles[i][:].rearrange("p g u r -> p g r u"))
+            nc.scalar.copy(out=grouped[:], in_=h_tiles[i][:].rearrange("p g u r -> p g r u"))
             h_words[i] = grouped
 
         def front_quantise(i):
@@ -230,8 +248,8 @@ def tile_qwen3block_pa_kernel(
         inv_rms = {}
 
         def multiply(job):
-            i, n = divmod(job, BANKS_PER_TILE)
-            acc = psum_o.tile([P, BANK], F32)
+            i, n = JOBS[job]
+            acc = psum_o.tile([P, BANK], F32, tag="bank")
             for g in range(PASSES):
                 nc.tensor.matmul_mx(
                     out=acc[:],
@@ -245,14 +263,14 @@ def tile_qwen3block_pa_kernel(
             banks[job] = acc
 
         def store(job, result):
-            i, n = divmod(job, BANKS_PER_TILE)
+            i, n = JOBS[job]
             rows = slice(P * i, P * (i + 1))
             if n < 2:
                 nc.sync.dma_start(out=q_rows[rows, BANK * n : BANK * (n + 1)], in_=result)
             elif n == 2:
                 nc.sync.dma_start(out=k_rows[rows, :], in_=result)
             else:
-                nc.sync.dma_start(out=v_rows[rows, :], in_=result)
+                nc.scalar.dma_start(out=v_rows[rows, :], in_=result)
 
         def copy_values(job):
             values = work.tile([P, BANK], F32)
@@ -278,7 +296,7 @@ def tile_qwen3block_pa_kernel(
             inv_rms[job] = head_inv_rms
 
         def rotate(job):
-            i, n = divmod(job, BANKS_PER_TILE)
+            i, n = JOBS[job]
             kind = n // 2
             half = i % 2
             head_inv_rms = inv_rms[job]
@@ -294,33 +312,47 @@ def tile_qwen3block_pa_kernel(
                 )
             result = work.tile([P, HEADS_PER_BANK * PAIRS, 2], F32)
             by_pair = products[:].rearrange("p h j m c -> p (h j) m c")
-            adder = nc.vector if kind == 1 else nc.gpsimd
+            adder = nc.vector if job == ROTATED_JOBS - 1 else nc.gpsimd
             adder.tensor_tensor(out=result[:], in0=by_pair[:, :, 0, :], in1=by_pair[:, :, 1, :], op=ALU.add)
             store(job, result[:].rearrange("p q c -> p (q c)"))
 
-        def is_rotated(job):
-            return 0 <= job < JOBS and job % BANKS_PER_TILE != VALUE_BANK
+        front_sum(0)
+        spread_gains()
+        front_sum(1)
+        front_scale(0)
+        front_transpose(0)
+        front_sum(2)
+        front_scale(1)
+        front_group(0)
+        front_transpose(1)
+        front_scale(2)
+        front_sum(3)
+        front_quantise(0)
+        for job in range(MATMUL_AHEAD):
+            multiply(job)
+        front_group(1)
+        front_scale(3)
+        front_quantise(1)
+        sum_squares(0)
+        invert_rms(0)
+        sum_squares(1)
 
-        for step in range(-FRONT_AHEAD, JOBS + ROTATE_BEHIND):
-            if 0 <= step + MATMUL_AHEAD < JOBS:
-                multiply(step + MATMUL_AHEAD)
-            for i in range(TILES):
-                first = BANKS_PER_TILE * i - FRONT_AHEAD
-                if step == first:
-                    front_sum(i)
-                if step == first + 2:
-                    front_scale_and_transpose(i)
-                if step == first + 3:
+        for step in range(len(JOBS)):
+            for i in range(2, TILES):
+                first = ROTATED_BANKS * i
+                if step == first - TRANSPOSE_AHEAD:
+                    front_transpose(i)
+                if step == first - GROUP_AHEAD:
                     front_group(i)
-                if step == first + 4:
+                if step == first - QUANTISE_AHEAD:
                     front_quantise(i)
-            if step == TABLES_STEP:
-                rotation_tables()
-            if is_rotated(step):
-                sum_squares(step)
-            elif 0 <= step < JOBS:
-                copy_values(step)
-            if is_rotated(step - INVERT_BEHIND):
-                invert_rms(step - INVERT_BEHIND)
-            if is_rotated(step - ROTATE_BEHIND):
-                rotate(step - ROTATE_BEHIND)
+            if step + MATMUL_AHEAD < len(JOBS):
+                multiply(step + MATMUL_AHEAD)
+            if step + SUM_AHEAD < ROTATED_JOBS:
+                sum_squares(step + SUM_AHEAD)
+            elif step + SUM_AHEAD < len(JOBS):
+                copy_values(step + SUM_AHEAD)
+            if step + INVERT_AHEAD < ROTATED_JOBS:
+                invert_rms(step + INVERT_AHEAD)
+            if step < ROTATED_JOBS:
+                rotate(step)

@@ -171,15 +171,12 @@ def tile_qwen3block_pa_kernel(
                         op=ALU.mult,
                     )
 
-        ln_w_all = []
+        ln_w_all = psum_o.tile([P, E], BF16, tag="bank")
 
         def spread_gains():
             for g in range(PASSES):
-                ln_w_bank = psum_o.tile([P, K_PASS], F32, tag="bank")
-                nc.tensor.matmul(
-                    out=ln_w_bank[:], lhsT=ones[:], rhs=gain_rows[:, K_PASS * g : K_PASS * (g + 1)], start=True, stop=True
-                )
-                ln_w_all.append(ln_w_bank)
+                k_cols = slice(K_PASS * g, K_PASS * (g + 1))
+                nc.tensor.matmul(out=ln_w_all[:, k_cols], lhsT=ones[:], rhs=gain_rows[:, k_cols], start=True, stop=True)
             head_w_bank = psum_t.tile([P, BANK], F32, tag="turned")
             nc.tensor.matmul(
                 out=head_w_bank[:, 0 : 2 * HD], lhsT=ones[:], rhs=gain_rows[:, E : E + 2 * HD], start=True, stop=True
@@ -213,12 +210,9 @@ def tile_qwen3block_pa_kernel(
 
         def front_scale(i):
             h = front.tile([P, E], BF16)
-            for g in range(PASSES):
-                k_cols = slice(K_PASS * g, K_PASS * (g + 1))
-                nc.vector.scalar_tensor_tensor(
-                    out=h[:, k_cols], in0=x_sb[:, i, k_cols], scalar=x_inv_rms_tiles[i][:], in1=ln_w_all[g][:],
-                    op0=ALU.mult, op1=ALU.mult,
-                )
+            nc.vector.scalar_tensor_tensor(
+                out=h[:], in0=x_sb[:, i, :], scalar=x_inv_rms_tiles[i][:], in1=ln_w_all[:], op0=ALU.mult, op1=ALU.mult
+            )
             h_rows[i] = h
 
         def front_transpose(i):
@@ -312,9 +306,20 @@ def tile_qwen3block_pa_kernel(
                 )
             result = work.tile([P, HEADS_PER_BANK * PAIRS, 2], F32)
             by_pair = products[:].rearrange("p h j m c -> p (h j) m c")
-            adder = nc.vector if job == ROTATED_JOBS - 1 else nc.gpsimd
-            adder.tensor_tensor(out=result[:], in0=by_pair[:, :, 0, :], in1=by_pair[:, :, 1, :], op=ALU.add)
-            store(job, result[:].rearrange("p q c -> p (q c)"))
+            if job < ROTATED_JOBS - 1:
+                nc.gpsimd.tensor_tensor(out=result[:], in0=by_pair[:, :, 0, :], in1=by_pair[:, :, 1, :], op=ALU.add)
+                store(job, result[:].rearrange("p q c -> p (q c)"))
+            else:
+                rows = slice(P * i, P * (i + 1))
+                for part in range(2):
+                    pairs = slice(BANK // 4 * part, BANK // 4 * (part + 1))
+                    nc.vector.tensor_tensor(
+                        out=result[:, pairs, :], in0=by_pair[:, pairs, 0, :], in1=by_pair[:, pairs, 1, :], op=ALU.add
+                    )
+                    nc.sync.dma_start(
+                        out=k_rows[rows, BANK // 2 * part : BANK // 2 * (part + 1)],
+                        in_=result[:, pairs, :].rearrange("p q c -> p (q c)"),
+                    )
 
         front_sum(0)
         spread_gains()

@@ -64,15 +64,18 @@ def tile_qwen3block_pa_kernel(
         w_scales = keep.tile([P, 2048], U8, align_bytes=64)
         head_w_all = keep.tile([P, 2, HD], BF16)
 
+        powers = keep.tile([P, 2, 8], F32)
+        nc.gpsimd.memset(powers[:], 1.0)
+        eps = keep.tile([P, 1], F32)
+        nc.gpsimd.memset(eps[:], EPS)
         gain_rows = keep.tile([P, E + 2 * HD], BF16)
-        nc.gpsimd.memset(gain_rows[:].bitcast(F32), 0.0)
-        ones = keep.tile([P, P], BF16)
-        nc.vector.memset(ones[:], 1.0)
-
-        position_i = keep.tile([P, 2], I32)
-        nc.gpsimd.iota(position_i[:], pattern=[[P, 2]], base=0, channel_multiplier=1)
+        nc.gpsimd.memset(gain_rows[:, 0:E].bitcast(F32), 0.0)
+        position = keep.tile([P, 2], F32)
+        nc.gpsimd.iota(
+            position[:], pattern=[[P, 2]], base=0, channel_multiplier=1, allow_small_or_imprecise_dtypes=True
+        )
+        nc.gpsimd.memset(gain_rows[:, E : E + 2 * HD].bitcast(F32), 0.0)
         nc.gpsimd.memset(w_scales[:].bitcast(F32), 0.0)
-
 
         def load_x(i):
             nc.sync.dma_start(out=x_sb[:, i, :], in_=x_rows[P * i : P * (i + 1), :])
@@ -85,11 +88,11 @@ def tile_qwen3block_pa_kernel(
 
         load_x(0)
         nc.sync.dma_start(out=gain_rows[0:1, 0:E], in_=ln_w.unsqueeze(0))
-        nc.sync.dma_start(out=gain_rows[0:1, E : E + HD], in_=q_norm_w.unsqueeze(0))
-        nc.sync.dma_start(out=gain_rows[0:1, E + HD : E + 2 * HD], in_=k_norm_w.unsqueeze(0))
         load_x(1)
         load_x(2)
         load_x(3)
+        nc.sync.dma_start(out=gain_rows[0:1, E : E + HD], in_=q_norm_w.unsqueeze(0))
+        nc.sync.dma_start(out=gain_rows[0:1, E + HD : E + 2 * HD], in_=k_norm_w.unsqueeze(0))
         for quadrant in range(4):
             nc.sync.dma_start(
                 out=w_scales[32 * quadrant : 32 * quadrant + 4 * PASSES, :].bitcast(I32),
@@ -103,58 +106,62 @@ def tile_qwen3block_pa_kernel(
         identity = keep.tile([P, P], F32)
         make_identity(nc, identity[:])
 
-        eps = keep.tile([P, 1], F32)
-        nc.vector.memset(eps[:], EPS)
         warm = keep.tile([P, 2], F32)
-        nc.scalar.activation(out=warm[:, 0:1], in_=eps[:], func=ACT.Sin)
-        coarse = keep.tile([P, 8], F32)
-        fine = keep.tile([P, 8], F32)
-        nc.vector.memset(coarse[:, 0:1], 1.0)
-        nc.vector.memset(fine[:, 0:1], 1.0)
+        nc.scalar.activation(out=warm[:, 0:1], in_=powers[:, 0, 0:1], func=ACT.Sin)
+        coarse = powers[:, 0, :]
+        fine = powers[:, 1, :]
+        for j_low in range(2):
+            nc.vector.tensor_scalar(
+                out=fine[:, j_low : j_low + 1], in0=coarse[:, 0:1],
+                scalar1=ROPE_BASE ** (-2.0 * j_low / HD) / (2.0 * math.pi), scalar2=None, op0=ALU.mult,
+            )
         for level in range(3):
             width = 2**level
             nc.vector.tensor_scalar(
                 out=coarse[:, width : 2 * width], in0=coarse[:, 0:width],
                 scalar1=ROPE_BASE ** (-16.0 * width / HD), scalar2=None, op0=ALU.mult,
             )
-            nc.vector.tensor_scalar(
-                out=fine[:, width : 2 * width], in0=fine[:, 0:width],
-                scalar1=ROPE_BASE ** (-2.0 * width / HD), scalar2=None, op0=ALU.mult,
-            )
-        position = keep.tile([P, 2], F32)
-        nc.vector.tensor_scalar(
-            out=position[:], in0=position_i[:], scalar1=1.0 / (2.0 * math.pi), scalar2=None, op0=ALU.mult
-        )
+            if level > 0:
+                nc.vector.tensor_scalar(
+                    out=fine[:, width : 2 * width], in0=fine[:, 0:width],
+                    scalar1=ROPE_BASE ** (-2.0 * width / HD), scalar2=None, op0=ALU.mult,
+                )
         turns = keep.tile([P, 2, 8, 8], F32)
         for half in range(2):
             nc.vector.scalar_tensor_tensor(
                 out=turns[:, half, :, :],
-                in0=coarse[:].unsqueeze(2).to_broadcast([P, 8, 8]),
+                in0=coarse.unsqueeze(2).to_broadcast([P, 8, 8]),
                 scalar=position[:, half : half + 1],
-                in1=fine[:].unsqueeze(1).to_broadcast([P, 8, 8]),
+                in1=fine.unsqueeze(1).to_broadcast([P, 8, 8]),
                 op0=ALU.mult,
                 op1=ALU.mult,
             )
-        shifted = keep.tile([P, 2, 8, 8], F32)
-        nc.vector.tensor_scalar(out=shifted[:], in0=turns[:], scalar1=ROUND_MAGIC, scalar2=None, op0=ALU.add)
-        sin_of = keep.tile([P, 2, 3, PAIRS], F32)
-        minus_part = sin_of[:, :, 0, :]
-        nc.vector.scalar_tensor_tensor(
-            out=minus_part, in0=shifted[:].rearrange("p b h l -> p b (h l)"), scalar=ROUND_MAGIC,
-            in1=turns[:].rearrange("p b h l -> p b (h l)"), op0=ALU.subtract, op1=ALU.subtract,
-        )
-        magnitude = keep.tile([P, 2, PAIRS], F32)
-        nc.vector.scalar_tensor_tensor(
-            out=magnitude[:], in0=minus_part, scalar=-1.0, in1=minus_part, op0=ALU.mult, op1=ALU.max
-        )
+        flat_turns = turns[:].rearrange("p b h l -> p (b h l)")
+        quarter_on = keep.tile([P, 2 * PAIRS], F32)
+        nc.vector.tensor_scalar(out=quarter_on[:], in0=flat_turns, scalar1=0.25, scalar2=None, op0=ALU.add)
+        shifted = keep.tile([P, 2, 2 * PAIRS], F32)
         nc.vector.tensor_scalar(
-            out=sin_of[:, :, 1, :], in0=magnitude[:], scalar1=-1.0, scalar2=0.25, op0=ALU.mult, op1=ALU.add
+            out=shifted[:, 0, :], in0=flat_turns, scalar1=0.25, scalar2=ROUND_MAGIC, op0=ALU.add, op1=ALU.add
         )
-        nc.vector.tensor_scalar(out=sin_of[:, :, 2, :], in0=minus_part, scalar1=-1.0, scalar2=None, op0=ALU.mult)
-        trig = keep.tile([P, 2, 3, PAIRS], F32)
+        nc.vector.tensor_scalar(out=shifted[:, 1, :], in0=flat_turns, scalar1=ROUND_MAGIC, scalar2=None, op0=ALU.add)
+        less_turns = keep.tile([P, 2, 2 * PAIRS], F32)
+        nc.vector.scalar_tensor_tensor(
+            out=less_turns[:, 0, :], in0=shifted[:, 0, :], scalar=ROUND_MAGIC, in1=quarter_on[:],
+            op0=ALU.subtract, op1=ALU.subtract,
+        )
+        nc.vector.scalar_tensor_tensor(
+            out=less_turns[:, 1, :], in0=shifted[:, 1, :], scalar=ROUND_MAGIC, in1=flat_turns,
+            op0=ALU.subtract, op1=ALU.subtract,
+        )
+        ones = keep.tile([P, P], BF16)
+        nc.vector.memset(ones[:], 1.0)
+        trig = keep.tile([P, 3, 2, PAIRS], F32)
         nc.scalar.activation(
-            out=trig[:].rearrange("p b c j -> p (b c j)"), in_=sin_of[:].rearrange("p b c j -> p (b c j)"),
-            func=ACT.Sin, scale=2.0 * math.pi,
+            out=trig[:, 1:3, :, :].rearrange("p c b j -> p (c b j)"), in_=less_turns[:].rearrange("p c q -> p (c q)"),
+            func=ACT.Sin, scale=-2.0 * math.pi,
+        )
+        nc.scalar.activation(
+            out=trig[:, 0, :, :].rearrange("p b j -> p (b j)"), in_=less_turns[:, 1, :], func=ACT.Sin, scale=2.0 * math.pi
         )
         nc.scalar.activation(out=warm[:, 1:2], in_=eps[:], func=ACT.Abs_reciprocal_sqrt)
 
@@ -166,7 +173,7 @@ def tile_qwen3block_pa_kernel(
                     gain = head_w_all[:, kind, :].rearrange("p (j e) -> p j e", e=2)[:, :, member]
                     nc.gpsimd.tensor_tensor(
                         out=table[:, kind, :, :, member, :],
-                        in0=trig[:, :, 1 - member : 3 - member, :].rearrange("p b c j -> p b j c"),
+                        in0=trig[:, 1 - member : 3 - member, :, :].rearrange("p c b j -> p b j c"),
                         in1=gain.unsqueeze(1).unsqueeze(3).to_broadcast([P, 2, PAIRS, 2]),
                         op=ALU.mult,
                     )

@@ -36,9 +36,10 @@ FLOPS = 2 * TOKENS * E * 2048
 MATMUL_AHEAD = 3
 SUM_AHEAD = 2
 INVERT_AHEAD = 1
-QUANTISE_AHEAD = 3
-GROUP_AHEAD = 4
-TRANSPOSE_AHEAD = 6
+LATE_TILES = (2, 3)
+LATE_QUANTISE_STEP = 3
+LATE_TRANSPOSE_STEP = {2: 0, 3: 1}
+LATE_GROUP_STEP = {2: 1, 3: 2}
 
 
 def tile_qwen3block_pa_kernel(
@@ -232,10 +233,25 @@ def tile_qwen3block_pa_kernel(
                     )
             h_tiles[i] = h_t
 
+        late_words = keep.tile([P, len(LATE_TILES), PASSES, P, 2], F32, align_bytes=64)
+
         def front_group(i):
+            if i in LATE_TILES:
+                nc.scalar.copy(
+                    out=late_words[:, i - LATE_TILES[0], :, :, :], in_=h_tiles[i][:].rearrange("p g u r -> p g r u")
+                )
+                return
             grouped = front.tile([P, PASSES, P, 2], F32, align_bytes=64)
             nc.scalar.copy(out=grouped[:], in_=h_tiles[i][:].rearrange("p g u r -> p g r u"))
             h_words[i] = grouped
+
+        def quantise_late_tiles():
+            first = LATE_TILES[0]
+            nc.vector.quantize_mx(
+                out=h_codes[:, first:TILES, :].rearrange("p i c -> p (i c)").bitcast(FP8X4),
+                scales=h_scales[:, first:TILES, :].rearrange("p i c -> p (i c)"),
+                in_=late_words[:].rearrange("p i g r u -> p (i g r u)").bitcast(BF16),
+            )
 
         def front_quantise(i):
             nc.vector.quantize_mx(
@@ -350,14 +366,13 @@ def tile_qwen3block_pa_kernel(
         sum_squares(1)
 
         for step in range(len(JOBS)):
-            for i in range(2, TILES):
-                first = ROTATED_BANKS * i
-                if step == first - TRANSPOSE_AHEAD:
+            for i in LATE_TILES:
+                if step == LATE_TRANSPOSE_STEP[i]:
                     front_transpose(i)
-                if step == first - GROUP_AHEAD:
+                if step == LATE_GROUP_STEP[i]:
                     front_group(i)
-                if step == first - QUANTISE_AHEAD:
-                    front_quantise(i)
+            if step == LATE_QUANTISE_STEP:
+                quantise_late_tiles()
             if step + MATMUL_AHEAD < len(JOBS):
                 multiply(step + MATMUL_AHEAD)
             if step + SUM_AHEAD < ROTATED_JOBS:

@@ -37,6 +37,7 @@ MATMUL_AHEAD = 3
 SUM_AHEAD = 2
 INVERT_AHEAD = 1
 LATE_TILES = (2, 3)
+VECTOR_ADDS = 2
 LATE_QUANTISE_STEP = 3
 LATE_TRANSPOSE_STEP = {2: 0, 3: 1}
 LATE_GROUP_STEP = {2: 1, 3: 2}
@@ -263,6 +264,7 @@ def tile_qwen3block_pa_kernel(
         banks = {}
         totals = {}
         inv_rms = {}
+        left_to_vector = {}
 
         def multiply(job):
             i, n = JOBS[job]
@@ -327,22 +329,29 @@ def tile_qwen3block_pa_kernel(
                     op0=ALU.mult,
                     op1=ALU.mult,
                 )
-            result = work.tile([P, HEADS_PER_BANK * PAIRS, 2], F32)
             by_pair = products[:].rearrange("p h j m c -> p (h j) m c")
-            if job < ROTATED_JOBS - 1:
+            if job < ROTATED_JOBS - VECTOR_ADDS:
+                result = work.tile([P, HEADS_PER_BANK * PAIRS, 2], F32)
                 nc.gpsimd.tensor_tensor(out=result[:], in0=by_pair[:, :, 0, :], in1=by_pair[:, :, 1, :], op=ALU.add)
                 store(job, result[:].rearrange("p q c -> p (q c)"))
             else:
-                rows = slice(P * i, P * (i + 1))
-                for part in range(2):
-                    pairs = slice(BANK // 4 * part, BANK // 4 * (part + 1))
-                    nc.vector.tensor_tensor(
-                        out=result[:, pairs, :], in0=by_pair[:, pairs, 0, :], in1=by_pair[:, pairs, 1, :], op=ALU.add
-                    )
-                    nc.sync.dma_start(
-                        out=k_rows[rows, BANK // 2 * part : BANK // 2 * (part + 1)],
-                        in_=result[:, pairs, :].rearrange("p q c -> p (q c)"),
-                    )
+                left_to_vector[job] = by_pair
+
+        def vector_add(job):
+            i, n = JOBS[job]
+            by_pair = left_to_vector[job]
+            result = work.tile([P, HEADS_PER_BANK * PAIRS, 2], F32)
+            rows = slice(P * i, P * (i + 1))
+            for part in range(2):
+                pairs = slice(BANK // 4 * part, BANK // 4 * (part + 1))
+                nc.vector.tensor_tensor(
+                    out=result[:, pairs, :], in0=by_pair[:, pairs, 0, :], in1=by_pair[:, pairs, 1, :], op=ALU.add
+                )
+                if n < 2:
+                    target = q_rows[rows, BANK * n + BANK // 2 * part : BANK * n + BANK // 2 * (part + 1)]
+                else:
+                    target = k_rows[rows, BANK // 2 * part : BANK // 2 * (part + 1)]
+                nc.sync.dma_start(out=target, in_=result[:, pairs, :].rearrange("p q c -> p (q c)"))
 
         front_sum(0)
         spread_gains()
@@ -383,3 +392,6 @@ def tile_qwen3block_pa_kernel(
                 invert_rms(step + INVERT_AHEAD)
             if step < ROTATED_JOBS:
                 rotate(step)
+            if step == ROTATED_JOBS - 1:
+                for job in range(ROTATED_JOBS - VECTOR_ADDS, ROTATED_JOBS):
+                    vector_add(job)

@@ -71,12 +71,11 @@ def tile_qwen3block_pa_kernel(
         eps = keep.tile([P, 1], F32)
         nc.gpsimd.memset(eps[:], EPS)
         gain_rows = keep.tile([P, E + 2 * HD], BF16)
-        nc.gpsimd.memset(gain_rows[:, 0:E].bitcast(F32), 0.0)
+        nc.gpsimd.memset(gain_rows[:].bitcast(F32), 0.0)
         position = keep.tile([P, 2], F32)
         nc.gpsimd.iota(
             position[:], pattern=[[P, 2]], base=0, channel_multiplier=1, allow_small_or_imprecise_dtypes=True
         )
-        nc.gpsimd.memset(gain_rows[:, E : E + 2 * HD].bitcast(F32), 0.0)
         nc.gpsimd.memset(w_scales[:].bitcast(F32), 0.0)
 
         def load_x(i):
@@ -90,11 +89,11 @@ def tile_qwen3block_pa_kernel(
 
         load_x(0)
         nc.sync.dma_start(out=gain_rows[0:1, 0:E], in_=ln_w.unsqueeze(0))
+        nc.sync.dma_start(out=gain_rows[0:1, E : E + HD], in_=q_norm_w.unsqueeze(0))
+        nc.sync.dma_start(out=gain_rows[0:1, E + HD : E + 2 * HD], in_=k_norm_w.unsqueeze(0))
         load_x(1)
         load_x(2)
         load_x(3)
-        nc.sync.dma_start(out=gain_rows[0:1, E : E + HD], in_=q_norm_w.unsqueeze(0))
-        nc.sync.dma_start(out=gain_rows[0:1, E + HD : E + 2 * HD], in_=k_norm_w.unsqueeze(0))
         for quadrant in range(4):
             nc.sync.dma_start(
                 out=w_scales[32 * quadrant : 32 * quadrant + 4 * PASSES, :].bitcast(I32),
@@ -107,6 +106,8 @@ def tile_qwen3block_pa_kernel(
 
         identity = keep.tile([P, P], F32)
         make_identity(nc, identity[:])
+        ones = keep.tile([P, P], BF16)
+        nc.vector.memset(ones[:], 1.0)
 
         warm = keep.tile([P, 2], F32)
         nc.scalar.activation(out=warm[:, 0:1], in_=powers[:, 0, 0:1], func=ACT.Sin)
@@ -155,8 +156,6 @@ def tile_qwen3block_pa_kernel(
             out=less_turns[:, 1, :], in0=shifted[:, 1, :], scalar=ROUND_MAGIC, in1=flat_turns,
             op0=ALU.subtract, op1=ALU.subtract,
         )
-        ones = keep.tile([P, P], BF16)
-        nc.vector.memset(ones[:], 1.0)
         trig = keep.tile([P, 3, 2, PAIRS], F32)
         nc.scalar.activation(
             out=trig[:, 1:3, :, :].rearrange("p c b j -> p (c b j)"), in_=less_turns[:].rearrange("p c q -> p (c q)"),

@@ -106,29 +106,25 @@ def tile_qwen3block_pa_kernel(
 
         identity = keep.tile([P, P], F32)
         make_identity(nc, identity[:])
-        ones = keep.tile([P, P], BF16)
-        nc.vector.memset(ones[:], 1.0)
 
         warm = keep.tile([P, 2], F32)
         nc.scalar.activation(out=warm[:, 0:1], in_=powers[:, 0, 0:1], func=ACT.Sin)
         coarse = powers[:, 0, :]
         fine = powers[:, 1, :]
+
+        def scaled(out, in0, factor):
+            nc.vector.scalar_tensor_tensor(out=out, in0=in0, scalar=factor, in1=in0, op0=ALU.mult, op1=ALU.min)
+
+        def raised(out, in0, addend):
+            nc.vector.scalar_tensor_tensor(out=out, in0=in0, scalar=addend, in1=in0, op0=ALU.add, op1=ALU.max)
+
         for j_low in range(2):
-            nc.vector.tensor_scalar(
-                out=fine[:, j_low : j_low + 1], in0=coarse[:, 0:1],
-                scalar1=ROPE_BASE ** (-2.0 * j_low / HD) / (2.0 * math.pi), scalar2=None, op0=ALU.mult,
-            )
+            scaled(fine[:, j_low : j_low + 1], coarse[:, 0:1], ROPE_BASE ** (-2.0 * j_low / HD) / (2.0 * math.pi))
         for level in range(3):
             width = 2**level
-            nc.vector.tensor_scalar(
-                out=coarse[:, width : 2 * width], in0=coarse[:, 0:width],
-                scalar1=ROPE_BASE ** (-16.0 * width / HD), scalar2=None, op0=ALU.mult,
-            )
+            scaled(coarse[:, width : 2 * width], coarse[:, 0:width], ROPE_BASE ** (-16.0 * width / HD))
             if level > 0:
-                nc.vector.tensor_scalar(
-                    out=fine[:, width : 2 * width], in0=fine[:, 0:width],
-                    scalar1=ROPE_BASE ** (-2.0 * width / HD), scalar2=None, op0=ALU.mult,
-                )
+                scaled(fine[:, width : 2 * width], fine[:, 0:width], ROPE_BASE ** (-2.0 * width / HD))
         turns = keep.tile([P, 2, 8, 8], F32)
         for half in range(2):
             nc.vector.scalar_tensor_tensor(
@@ -141,29 +137,27 @@ def tile_qwen3block_pa_kernel(
             )
         flat_turns = turns[:].rearrange("p b h l -> p (b h l)")
         quarter_on = keep.tile([P, 2 * PAIRS], F32)
-        nc.vector.tensor_scalar(out=quarter_on[:], in0=flat_turns, scalar1=0.25, scalar2=None, op0=ALU.add)
         shifted = keep.tile([P, 2, 2 * PAIRS], F32)
-        nc.vector.tensor_scalar(
-            out=shifted[:, 0, :], in0=flat_turns, scalar1=0.25, scalar2=ROUND_MAGIC, op0=ALU.add, op1=ALU.add
-        )
-        nc.vector.tensor_scalar(out=shifted[:, 1, :], in0=flat_turns, scalar1=ROUND_MAGIC, scalar2=None, op0=ALU.add)
         less_turns = keep.tile([P, 2, 2 * PAIRS], F32)
-        nc.vector.scalar_tensor_tensor(
-            out=less_turns[:, 0, :], in0=shifted[:, 0, :], scalar=ROUND_MAGIC, in1=quarter_on[:],
-            op0=ALU.subtract, op1=ALU.subtract,
-        )
+        raised(shifted[:, 1, :], flat_turns, ROUND_MAGIC)
+        raised(quarter_on[:], flat_turns, 0.25)
         nc.vector.scalar_tensor_tensor(
             out=less_turns[:, 1, :], in0=shifted[:, 1, :], scalar=ROUND_MAGIC, in1=flat_turns,
             op0=ALU.subtract, op1=ALU.subtract,
         )
+        raised(shifted[:, 0, :], quarter_on[:], ROUND_MAGIC)
+        nc.vector.scalar_tensor_tensor(
+            out=less_turns[:, 0, :], in0=shifted[:, 0, :], scalar=ROUND_MAGIC, in1=quarter_on[:],
+            op0=ALU.subtract, op1=ALU.subtract,
+        )
+        ones = keep.tile([P, P], BF16)
+        nc.vector.memset(ones[:], 1.0)
         trig = keep.tile([P, 3, 2, PAIRS], F32)
-        nc.scalar.activation(
-            out=trig[:, 1:3, :, :].rearrange("p c b j -> p (c b j)"), in_=less_turns[:].rearrange("p c q -> p (c q)"),
-            func=ACT.Sin, scale=-2.0 * math.pi,
-        )
-        nc.scalar.activation(
-            out=trig[:, 0, :, :].rearrange("p b j -> p (b j)"), in_=less_turns[:, 1, :], func=ACT.Sin, scale=2.0 * math.pi
-        )
+        for plane, reduced, sign in ((2, 1, -1.0), (0, 1, 1.0), (1, 0, -1.0)):
+            nc.scalar.activation(
+                out=trig[:, plane, :, :].rearrange("p b j -> p (b j)"), in_=less_turns[:, reduced, :], func=ACT.Sin,
+                scale=sign * 2.0 * math.pi,
+            )
         nc.scalar.activation(out=warm[:, 1:2], in_=eps[:], func=ACT.Abs_reciprocal_sqrt)
 
         table = keep.tile([P, 2, 2, PAIRS, 2, 2], F32)

@@ -68,14 +68,14 @@ def tile_qwen3block_pa_kernel(
 
         powers = keep.tile([P, 2, 8], F32)
         nc.gpsimd.memset(powers[:], 1.0)
-        eps = keep.tile([P, 1], F32)
-        nc.gpsimd.memset(eps[:], EPS)
         gain_rows = keep.tile([P, E + 2 * HD], BF16)
         nc.gpsimd.memset(gain_rows[:].bitcast(F32), 0.0)
         position = keep.tile([P, 2], F32)
         nc.gpsimd.iota(
             position[:], pattern=[[P, 2]], base=0, channel_multiplier=1, allow_small_or_imprecise_dtypes=True
         )
+        eps = keep.tile([P, 1], F32)
+        nc.gpsimd.memset(eps[:], EPS)
         nc.gpsimd.memset(w_scales[:].bitcast(F32), 0.0)
 
         def load_x(i):
@@ -120,6 +120,8 @@ def tile_qwen3block_pa_kernel(
 
         for j_low in range(2):
             scaled(fine[:, j_low : j_low + 1], coarse[:, 0:1], ROPE_BASE ** (-2.0 * j_low / HD) / (2.0 * math.pi))
+        ones = keep.tile([P, P], BF16)
+        raised(ones[:], coarse[:, 0:1].to_broadcast([P, P]), 0.0)
         for level in range(3):
             width = 2**level
             scaled(coarse[:, width : 2 * width], coarse[:, 0:width], ROPE_BASE ** (-16.0 * width / HD))
@@ -150,8 +152,6 @@ def tile_qwen3block_pa_kernel(
             out=less_turns[:, 0, :], in0=shifted[:, 0, :], scalar=ROUND_MAGIC, in1=quarter_on[:],
             op0=ALU.subtract, op1=ALU.subtract,
         )
-        ones = keep.tile([P, P], BF16)
-        nc.vector.memset(ones[:], 1.0)
         trig = keep.tile([P, 3, 2, PAIRS], F32)
         for plane, reduced, sign in ((2, 1, -1.0), (0, 1, 1.0), (1, 0, -1.0)):
             nc.scalar.activation(
@@ -185,6 +185,12 @@ def tile_qwen3block_pa_kernel(
             )
             nc.vector.tensor_copy(out=head_w_all[:].rearrange("p k d -> p (k d)"), in_=head_w_bank[:, 0 : 2 * HD])
             rotation_tables()
+
+        idle_bank = psum_o.tile([P, BANK], F32, tag="bank")
+
+        def keep_warm(i, count):
+            for repeat in range(count):
+                nc.tensor.matmul(out=idle_bank[:], lhsT=ones[:], rhs=x_sb[:, i, 0:BANK], start=True, stop=True)
 
         h_codes = keep.tile([P, TILES, PASSES * P], U32, align_bytes=64)
         h_scales = keep.tile([P, TILES, PASSES * P], U8, align_bytes=64)
@@ -348,13 +354,16 @@ def tile_qwen3block_pa_kernel(
 
         front_sum(0)
         spread_gains()
+        keep_warm(0, 2)
         front_sum(1)
         front_scale(0)
         front_transpose(0)
+        keep_warm(1, 2)
         front_sum(2)
         front_scale(1)
         front_group(0)
         front_transpose(1)
+        keep_warm(2, 1)
         front_scale(2)
         front_sum(3)
         front_quantise(0)

@@ -63,7 +63,7 @@ def tile_qwen3block_pa_kernel(
 
         x_sb = keep.tile([P, TILES, E], BF16)
         w_words = keep.tile([P, PASSES, 2048], U32, align_bytes=64)
-        w_scales = keep.tile([P, 2048], U8, align_bytes=64)
+        w_scales = keep.tile([P, PASSES, 2048], U8, align_bytes=64)
         head_w_all = keep.tile([P, 2, HD], BF16)
 
         powers = keep.tile([P, 2, 8], F32)
@@ -76,7 +76,6 @@ def tile_qwen3block_pa_kernel(
         )
         eps = keep.tile([P, 1], F32)
         nc.gpsimd.memset(eps[:], EPS)
-        nc.gpsimd.memset(w_scales[:].bitcast(F32), 0.0)
 
         def load_x(i):
             nc.sync.dma_start(out=x_sb[:, i, :], in_=x_rows[P * i : P * (i + 1), :])
@@ -94,11 +93,15 @@ def tile_qwen3block_pa_kernel(
         load_x(1)
         load_x(2)
         load_x(3)
-        for quadrant in range(4):
-            nc.sync.dma_start(
-                out=w_scales[32 * quadrant : 32 * quadrant + 4 * PASSES, :].bitcast(I32),
-                in_=qkv_w_scales[:, 4 * quadrant : 4 * quadrant + 4, :].bitcast(I32),
-            )
+        for g in range(PASSES):
+            for quadrant in range(4):
+                nc.sync.dma_start(
+                    out=w_scales[32 * quadrant : 32 * (quadrant + 1), g, :].bitcast(I32),
+                    in_=qkv_w_scales[g, 4 * quadrant : 4 * quadrant + 4, :]
+                    .bitcast(I32)
+                    .unsqueeze(0)
+                    .to_broadcast([8, 4, 2048 // 4]),
+                )
         load_w(0)
         load_w(1)
         load_w(2)
@@ -274,7 +277,7 @@ def tile_qwen3block_pa_kernel(
                     lhsT=h_codes[:, i, P * g : P * (g + 1)].bitcast(FP8X4),
                     lhsT_scale=h_scales[:, i, P * g : P * (g + 1)],
                     rhs=w_words[:, g, BANK * n : BANK * (n + 1)].bitcast(FP8X4),
-                    rhs_scale=w_scales[4 * g : P, BANK * n : BANK * (n + 1)],
+                    rhs_scale=w_scales[:, g, BANK * n : BANK * (n + 1)],
                     start=(g == 0),
                     stop=(g == PASSES - 1),
                 )

@@ -156,23 +156,23 @@ def tile_qwen3block_pa_kernel(
             op0=ALU.subtract, op1=ALU.subtract,
         )
         trig = keep.tile([P, 3, 2, PAIRS], F32)
-        for plane, reduced, sign in ((2, 1, -1.0), (0, 1, 1.0), (1, 0, -1.0)):
+        for plane, reduced, sign in ((0, 1, -1.0), (2, 1, 1.0), (1, 0, -1.0)):
             nc.scalar.activation(
                 out=trig[:, plane, :, :].rearrange("p b j -> p (b j)"), in_=less_turns[:, reduced, :], func=ACT.Sin,
                 scale=sign * 2.0 * math.pi,
             )
         nc.scalar.activation(out=warm[:, 1:2], in_=eps[:], func=ACT.Abs_reciprocal_sqrt)
 
-        table = keep.tile([P, 2, 2, PAIRS, 2, 2], F32)
+        table = keep.tile([P, 2, 2, 2, HD], F32)
 
         def rotation_tables():
             for kind in range(2):
-                for member in range(2):
-                    gain = head_w_all[:, kind, :].rearrange("p (j e) -> p j e", e=2)[:, :, member]
+                gain = head_w_all[:, kind, :].rearrange("p (j m) -> p j m", m=2)
+                for c in range(2):
                     nc.gpsimd.tensor_tensor(
-                        out=table[:, kind, :, :, member, :],
-                        in0=trig[:, 1 - member : 3 - member, :, :].rearrange("p c b j -> p b j c"),
-                        in1=gain.unsqueeze(1).unsqueeze(3).to_broadcast([P, 2, PAIRS, 2]),
+                        out=table[:, kind, :, c, :].rearrange("p b (j m) -> p b j m", m=2),
+                        in0=trig[:, 1 - c : 3 - c, :, :].rearrange("p m b j -> p b j m"),
+                        in1=gain.unsqueeze(1).to_broadcast([P, 2, PAIRS, 2]),
                         op=ALU.mult,
                     )
 
@@ -327,7 +327,7 @@ def tile_qwen3block_pa_kernel(
                     out=products[:, head, :, :, :].rearrange("p j m c -> p (j m) c"),
                     in0=banks[job][:, HD * head : HD * (head + 1)].unsqueeze(2).to_broadcast([P, HD, 2]),
                     scalar=head_inv_rms[:, head : head + 1],
-                    in1=table[:, kind, half, :, :, :].rearrange("p j m c -> p (j m) c"),
+                    in1=table[:, kind, half, :, :].rearrange("p c q -> p q c"),
                     op0=ALU.mult,
                     op1=ALU.mult,
                 )

import math
from contextlib import ExitStack

import concourse.mybir as mybir
from concourse.masks import make_identity

F32 = mybir.dt.float32
BF16 = mybir.dt.bfloat16
I32 = mybir.dt.int32
U32 = mybir.dt.uint32
U8 = mybir.dt.uint8
FP8X4 = mybir.dt.float8_e4m3fn_x4
ALU = mybir.AluOpType
ACT = mybir.ActivationFunctionType

P = 128
TOKENS = 512
E = 1024
HD = 128
PAIRS = HD // 2
K_PASS = 512
PASSES = E // K_PASS
BANK = 512
HEADS_PER_BANK = BANK // HD
ROTATED_BANKS = 3
VALUE_BANK = 3
TILES = TOKENS // P
JOBS = [(i, n) for i in range(TILES) for n in range(ROTATED_BANKS)] + [(i, VALUE_BANK) for i in range(TILES)]
ROTATED_JOBS = TILES * ROTATED_BANKS
EPS = 1e-6
ROPE_BASE = 1000000.0
ROUND_MAGIC = 12582912.0

FLOPS = 2 * TOKENS * E * 2048

MATMUL_AHEAD = 3
SUM_AHEAD = 2
INVERT_AHEAD = 1
LATE_TILES = (2, 3)
VECTOR_ADDS = 2
LATE_QUANTISE_STEP = 3
LATE_TRANSPOSE_STEP = {2: 0, 3: 1}
LATE_GROUP_STEP = {2: 1, 3: 2}


def tile_qwen3block_pa_kernel(
    tc, x, ln_w, qkv_w_words, qkv_w_scales, q_norm_w, k_norm_w, out_0, out_1, out_2
):
    nc = tc.nc
    x_rows = x.flatten_outer_dims()
    q_rows = out_0.rearrange("b s h d -> (b s) (h d)")
    k_rows = out_1.rearrange("b s h d -> (b s) (h d)")
    v_rows = out_2.rearrange("b s h d -> (b s) (h d)")

    with ExitStack() as stack:
        stack.enter_context(tc.manual_schedule())
        keep = stack.enter_context(tc.tile_pool(name="keep", bufs=1))
        front = stack.enter_context(tc.tile_pool(name="front", bufs=TILES))
        small = stack.enter_context(tc.tile_pool(name="small", bufs=8))
        work = stack.enter_context(tc.tile_pool(name="work", bufs=6))
        psum_t = stack.enter_context(tc.psum_pool(name="psum_t", bufs=1))
        psum_o = stack.enter_context(tc.psum_pool(name="psum_o", bufs=7))

        x_sb = keep.tile([P, TILES, E], BF16)
        w_words = keep.tile([P, PASSES, 2048], U32, align_bytes=64)
        w_scales = keep.tile([P, PASSES, 2048], U8, align_bytes=64)
        head_w_all = keep.tile([P, 2, HD], BF16)

        powers = keep.tile([P, 2, 8], F32)
        nc.gpsimd.memset(powers[:], 1.0)
        gain_rows = keep.tile([P, E + 2 * HD], BF16)
        nc.gpsimd.memset(gain_rows[:].bitcast(F32), 0.0)
        position = keep.tile([P, 2], F32)
        nc.gpsimd.iota(
            position[:], pattern=[[P, 2]], base=0, channel_multiplier=1, allow_small_or_imprecise_dtypes=True
        )
        eps = keep.tile([P, 1], F32)
        nc.gpsimd.memset(eps[:], EPS)

        def load_x(i):
            nc.sync.dma_start(out=x_sb[:, i, :], in_=x_rows[P * i : P * (i + 1), :])

        def load_w(n):
            nc.sync.dma_start(
                out=w_words[:, :, BANK * n : BANK * (n + 1)].bitcast(I32),
                in_=qkv_w_words.rearrange("g p n t -> p g (n t)")[:, :, 4 * BANK * n : 4 * BANK * (n + 1)].bitcast(I32),
            )

        load_x(0)
        nc.sync.dma_start(out=gain_rows[0:1, 0:E], in_=ln_w.unsqueeze(0))
        nc.sync.dma_start(out=gain_rows[0:1, E : E + HD], in_=q_norm_w.unsqueeze(0))
        nc.sync.dma_start(out=gain_rows[0:1, E + HD : E + 2 * HD], in_=k_norm_w.unsqueeze(0))
        load_x(1)
        load_x(2)
        load_x(3)
        for g in range(PASSES):
            for quadrant in range(4):
                nc.sync.dma_start(
                    out=w_scales[32 * quadrant : 32 * (quadrant + 1), g, :].bitcast(I32),
                    in_=qkv_w_scales[g, 4 * quadrant : 4 * quadrant + 4, :]
                    .bitcast(I32)
                    .unsqueeze(0)
                    .to_broadcast([8, 4, 2048 // 4]),
                )
        load_w(0)
        load_w(1)
        load_w(2)
        load_w(3)

        identity = keep.tile([P, P], F32)
        make_identity(nc, identity[:])

        warm = keep.tile([P, 2], F32)
        nc.scalar.activation(out=warm[:, 0:1], in_=powers[:, 0, 0:1], func=ACT.Sin)
        coarse = powers[:, 0, :]
        fine = powers[:, 1, :]

        def scaled(out, in0, factor):
            nc.vector.scalar_tensor_tensor(out=out, in0=in0, scalar=factor, in1=in0, op0=ALU.mult, op1=ALU.min)

        def raised(out, in0, addend):
            nc.vector.scalar_tensor_tensor(out=out, in0=in0, scalar=addend, in1=in0, op0=ALU.add, op1=ALU.max)

        for j_low in range(2):
            scaled(fine[:, j_low : j_low + 1], coarse[:, 0:1], ROPE_BASE ** (-2.0 * j_low / HD) / (2.0 * math.pi))
        ones = keep.tile([P, P], BF16)
        raised(ones[:], coarse[:, 0:1].to_broadcast([P, P]), 0.0)
        for level in range(3):
            width = 2**level
            scaled(coarse[:, width : 2 * width], coarse[:, 0:width], ROPE_BASE ** (-16.0 * width / HD))
            if level > 0:
                scaled(fine[:, width : 2 * width], fine[:, 0:width], ROPE_BASE ** (-2.0 * width / HD))
        turns = keep.tile([P, 2, 8, 8], F32)
        for half in range(2):
            nc.vector.scalar_tensor_tensor(
                out=turns[:, half, :, :],
                in0=coarse.unsqueeze(2).to_broadcast([P, 8, 8]),
                scalar=position[:, half : half + 1],
                in1=fine.unsqueeze(1).to_broadcast([P, 8, 8]),
                op0=ALU.mult,
                op1=ALU.mult,
            )
        flat_turns = turns[:].rearrange("p b h l -> p (b h l)")
        quarter_on = keep.tile([P, 2 * PAIRS], F32)
        shifted = keep.tile([P, 2, 2 * PAIRS], F32)
        less_turns = keep.tile([P, 2, 2 * PAIRS], F32)
        raised(shifted[:, 1, :], flat_turns, ROUND_MAGIC)
        raised(quarter_on[:], flat_turns, 0.25)
        nc.vector.scalar_tensor_tensor(
            out=less_turns[:, 1, :], in0=shifted[:, 1, :], scalar=ROUND_MAGIC, in1=flat_turns,
            op0=ALU.subtract, op1=ALU.subtract,
        )
        raised(shifted[:, 0, :], quarter_on[:], ROUND_MAGIC)
        nc.vector.scalar_tensor_tensor(
            out=less_turns[:, 0, :], in0=shifted[:, 0, :], scalar=ROUND_MAGIC, in1=quarter_on[:],
            op0=ALU.subtract, op1=ALU.subtract,
        )
        trig = keep.tile([P, 3, 2, PAIRS], F32)
        for plane, reduced, sign in ((0, 1, -1.0), (2, 1, 1.0), (1, 0, -1.0)):
            nc.scalar.activation(
                out=trig[:, plane, :, :].rearrange("p b j -> p (b j)"), in_=less_turns[:, reduced, :], func=ACT.Sin,
                scale=sign * 2.0 * math.pi,
            )
        nc.scalar.activation(out=warm[:, 1:2], in_=eps[:], func=ACT.Abs_reciprocal_sqrt)

        table = keep.tile([P, 2, 2, 2, HD], F32)

        def rotation_tables():
            for kind in range(2):
                gain = head_w_all[:, kind, :].rearrange("p (j m) -> p j m", m=2)
                for c in range(2):
                    nc.gpsimd.tensor_tensor(
                        out=table[:, kind, :, c, :].rearrange("p b (j m) -> p b j m", m=2),
                        in0=trig[:, 1 - c : 3 - c, :, :].rearrange("p m b j -> p b j m"),
                        in1=gain.unsqueeze(1).to_broadcast([P, 2, PAIRS, 2]),
                        op=ALU.mult,
                    )

        ln_w_all = psum_o.tile([P, E], BF16, tag="bank")

        def spread_gains():
            for g in range(PASSES):
                k_cols = slice(K_PASS * g, K_PASS * (g + 1))
                nc.tensor.matmul(out=ln_w_all[:, k_cols], lhsT=ones[:], rhs=gain_rows[:, k_cols], start=True, stop=True)
            head_w_bank = psum_t.tile([P, BANK], F32, tag="turned")
            nc.tensor.matmul(
                out=head_w_bank[:, 0 : 2 * HD], lhsT=ones[:], rhs=gain_rows[:, E : E + 2 * HD], start=True, stop=True
            )
            nc.vector.tensor_copy(out=head_w_all[:].rearrange("p k d -> p (k d)"), in_=head_w_bank[:, 0 : 2 * HD])
            rotation_tables()

        idle_bank = psum_o.tile([P, BANK], F32, tag="bank")

        def keep_warm(i, count):
            for repeat in range(count):
                nc.tensor.matmul(out=idle_bank[:], lhsT=ones[:], rhs=x_sb[:, i, 0:BANK], start=True, stop=True)

        h_codes = keep.tile([P, TILES, PASSES * P], U32, align_bytes=64)
        h_scales = keep.tile([P, TILES, PASSES * P], U8, align_bytes=64)
        x_inv_rms_tiles = {}
        h_tiles = {}
        h_words = {}

        def front_sum(i):
            x_squares = work.tile([P, E], BF16)
            x_total = small.tile([P, 1], F32)
            if i == 0:
                nc.vector.scalar_tensor_tensor(
                    out=x_squares[:], in0=x_sb[:, i, :], scalar=1.0, in1=x_sb[:, i, :], op0=ALU.mult, op1=ALU.mult,
                    accum_out=x_total[:],
                )
            else:
                nc.scalar.activation(out=x_squares[:], in_=x_sb[:, i, :], func=ACT.Square, accum_out=x_total[:])
            x_inv_rms = small.tile([P, 1], F32)
            nc.scalar.activation(
                out=x_inv_rms[:], in_=x_total[:], func=ACT.Abs_reciprocal_sqrt, scale=1.0 / E, bias=eps[:]
            )
            x_inv_rms_tiles[i] = x_inv_rms

        h_rows = {}

        def front_scale(i):
            h = front.tile([P, E], BF16)
            nc.vector.scalar_tensor_tensor(
                out=h[:], in0=x_sb[:, i, :], scalar=x_inv_rms_tiles[i][:], in1=ln_w_all[:], op0=ALU.mult, op1=ALU.mult
            )
            h_rows[i] = h

        def front_transpose(i):
            h = h_rows[i]
            h_t = psum_t.tile([P, PASSES, 2, P], F32, tag="turned")
            for g in range(PASSES):
                for u in range(2):
                    nc.tensor.transpose(
                        h_t[:, g, u, :], h[:].bitcast(F32)[:, 256 * g + u : 256 * (g + 1) : 2], identity[:]
                    )
            h_tiles[i] = h_t

        late_words = keep.tile([P, len(LATE_TILES), PASSES, P, 2], F32, align_bytes=64)

        def front_group(i):
            if i in LATE_TILES:
                nc.scalar.copy(
                    out=late_words[:, i - LATE_TILES[0], :, :, :], in_=h_tiles[i][:].rearrange("p g u r -> p g r u")
                )
                return
            grouped = front.tile([P, PASSES, P, 2], F32, align_bytes=64)
            nc.scalar.copy(out=grouped[:], in_=h_tiles[i][:].rearrange("p g u r -> p g r u"))
            h_words[i] = grouped

        def quantise_late_tiles():
            first = LATE_TILES[0]
            nc.vector.quantize_mx(
                out=h_codes[:, first:TILES, :].rearrange("p i c -> p (i c)").bitcast(FP8X4),
                scales=h_scales[:, first:TILES, :].rearrange("p i c -> p (i c)"),
                in_=late_words[:].rearrange("p i g r u -> p (i g r u)").bitcast(BF16),
            )

        def front_quantise(i):
            nc.vector.quantize_mx(
                out=h_codes[:, i, :].bitcast(FP8X4),
                scales=h_scales[:, i, :],
                in_=h_words[i][:].rearrange("p g r u -> p (g r u)").bitcast(BF16),
            )

        banks = {}
        totals = {}
        inv_rms = {}
        left_to_vector = {}

        def multiply(job):
            i, n = JOBS[job]
            acc = psum_o.tile([P, BANK], F32, tag="bank")
            for g in range(PASSES):
                nc.tensor.matmul_mx(
                    out=acc[:],
                    lhsT=h_codes[:, i, P * g : P * (g + 1)].bitcast(FP8X4),
                    lhsT_scale=h_scales[:, i, P * g : P * (g + 1)],
                    rhs=w_words[:, g, BANK * n : BANK * (n + 1)].bitcast(FP8X4),
                    rhs_scale=w_scales[:, g, BANK * n : BANK * (n + 1)],
                    start=(g == 0),
                    stop=(g == PASSES - 1),
                )
            banks[job] = acc

        def store(job, result):
            i, n = JOBS[job]
            rows = slice(P * i, P * (i + 1))
            if n < 2:
                nc.sync.dma_start(out=q_rows[rows, BANK * n : BANK * (n + 1)], in_=result)
            elif n == 2:
                nc.sync.dma_start(out=k_rows[rows, :], in_=result)
            else:
                nc.scalar.dma_start(out=v_rows[rows, :], in_=result)

        def copy_values(job):
            values = work.tile([P, BANK], F32)
            nc.scalar.copy(out=values[:], in_=banks[job][:])
            store(job, values[:])

        def sum_squares(job):
            acc = banks[job]
            head_squares = work.tile([P, HEADS_PER_BANK, HD], BF16)
            head_totals = small.tile([P, HEADS_PER_BANK], F32)
            for head in range(HEADS_PER_BANK):
                nc.scalar.activation(
                    out=head_squares[:, head, :], in_=acc[:, HD * head : HD * (head + 1)], func=ACT.Square,
                    accum_out=head_totals[:, head : head + 1],
                )
            totals[job] = head_totals

        def invert_rms(job):
            head_inv_rms = small.tile([P, HEADS_PER_BANK], F32)
            nc.scalar.activation(
                out=head_inv_rms[:], in_=totals[job][:], func=ACT.Abs_reciprocal_sqrt, scale=1.0 / HD, bias=eps[:]
            )
            inv_rms[job] = head_inv_rms

        def rotate(job):
            i, n = JOBS[job]
            kind = n // 2
            half = i % 2
            head_inv_rms = inv_rms[job]
            products = work.tile([P, HEADS_PER_BANK, PAIRS, 2, 2], F32)
            for head in range(HEADS_PER_BANK):
                nc.vector.scalar_tensor_tensor(
                    out=products[:, head, :, :, :].rearrange("p j m c -> p (j m) c"),
                    in0=banks[job][:, HD * head : HD * (head + 1)].unsqueeze(2).to_broadcast([P, HD, 2]),
                    scalar=head_inv_rms[:, head : head + 1],
                    in1=table[:, kind, half, :, :].rearrange("p c q -> p q c"),
                    op0=ALU.mult,
                    op1=ALU.mult,
                )
            by_pair = products[:].rearrange("p h j m c -> p (h j) m c")
            if job < ROTATED_JOBS - VECTOR_ADDS:
                result = work.tile([P, HEADS_PER_BANK * PAIRS, 2], F32)
                nc.gpsimd.tensor_tensor(out=result[:], in0=by_pair[:, :, 0, :], in1=by_pair[:, :, 1, :], op=ALU.add)
                store(job, result[:].rearrange("p q c -> p (q c)"))
            else:
                left_to_vector[job] = by_pair

        def vector_add(job):
            i, n = JOBS[job]
            by_pair = left_to_vector[job]
            result = work.tile([P, HEADS_PER_BANK * PAIRS, 2], F32)
            rows = slice(P * i, P * (i + 1))
            for part in range(2):
                pairs = slice(BANK // 4 * part, BANK // 4 * (part + 1))
                nc.vector.tensor_tensor(
                    out=result[:, pairs, :], in0=by_pair[:, pairs, 0, :], in1=by_pair[:, pairs, 1, :], op=ALU.add
                )
                if n < 2:
                    target = q_rows[rows, BANK * n + BANK // 2 * part : BANK * n + BANK // 2 * (part + 1)]
                else:
                    target = k_rows[rows, BANK // 2 * part : BANK // 2 * (part + 1)]
                nc.sync.dma_start(out=target, in_=result[:, pairs, :].rearrange("p q c -> p (q c)"))

        front_sum(0)
        spread_gains()
        keep_warm(0, 2)
        front_sum(1)
        front_scale(0)
        front_transpose(0)
        keep_warm(1, 2)
        front_sum(2)
        front_scale(1)
        front_group(0)
        front_transpose(1)
        keep_warm(2, 1)
        front_scale(2)
        front_sum(3)
        front_quantise(0)
        for job in range(MATMUL_AHEAD):
            multiply(job)
        front_group(1)
        front_scale(3)
        front_quantise(1)
        sum_squares(0)
        invert_rms(0)
        sum_squares(1)

        for step in range(len(JOBS)):
            for i in LATE_TILES:
                if step == LATE_TRANSPOSE_STEP[i]:
                    front_transpose(i)
                if step == LATE_GROUP_STEP[i]:
                    front_group(i)
            if step == LATE_QUANTISE_STEP:
                quantise_late_tiles()
            if step + MATMUL_AHEAD < len(JOBS):
                multiply(step + MATMUL_AHEAD)
            if step + SUM_AHEAD < ROTATED_JOBS:
                sum_squares(step + SUM_AHEAD)
            elif step + SUM_AHEAD < len(JOBS):
                copy_values(step + SUM_AHEAD)
            if step + INVERT_AHEAD < ROTATED_JOBS:
                invert_rms(step + INVERT_AHEAD)
            if step < ROTATED_JOBS:
                rotate(step)
            if step == ROTATED_JOBS - 1:
                for job in range(ROTATED_JOBS - VECTOR_ADDS, ROTATED_JOBS):
                    vector_add(job)
